import numpy as np
import ml_dtypes


def mxq(x, axis, fmt="e4m3"):
    dtype, down = {"e4m3": (ml_dtypes.float8_e4m3fn, 7), "e5m2": (ml_dtypes.float8_e5m2, 14)}[fmt]
    v = np.moveaxis(np.asarray(x, np.float32).astype(ml_dtypes.bfloat16).astype(np.float64), axis, -1)
    blocks = v.reshape(v.shape[:-1] + (-1, 32))
    amax = np.abs(blocks).max(-1, keepdims=True)
    byte = np.maximum(np.where(amax > 0, np.frexp(amax)[1] - 1 + 127, 0) - down, 1)
    scale = np.exp2(byte - 127.0)
    codes = (blocks / scale).astype(np.float32).astype(dtype).astype(np.float64)
    return np.moveaxis((codes * scale).reshape(v.shape), -1, axis)


WIDE = False


def mx_kscale(k):
    if not WIDE:
        return np.ones(k)
    levels = np.array([10, -10, 5, -5, 0])
    a = np.random.permutation(np.resize(levels, k // 512 * 4)).reshape(k // 512, 4)
    idx = np.arange(k)
    return np.exp2(a[idx // 512, idx % 128 // 32])


BF16 = ml_dtypes.bfloat16


def bf(x):
    return np.asarray(x, np.float32).astype(BF16)


def f64(x):
    return np.asarray(x).astype(np.float64)


E2M1 = np.array([0.0, 0.5, 1.0, 1.5, 2.0, 3.0, 4.0, 6.0, -0.0, -0.5, -1.0, -1.5, -2.0, -3.0, -4.0, -6.0])


def pack_weight(w, fmt):
    k, n = w.shape
    w = f64(bf(w)).reshape(k // 32, 32, n)
    amax = np.abs(w).max(1)
    if fmt == "e4m3":
        byte = np.frexp(amax)[1] - 1 + 127 - 7
    else:
        mant, ex = np.frexp(amax / 6.0)
        byte = np.where(mant > 0.5, ex, ex - 1) + 127
    byte = np.clip(np.where(amax > 0, byte, 1), 1, 254)
    scaled = (w * np.exp2(127.0 - byte)[:, None, :]).reshape(k, n).astype(np.float32)
    by_word = np.ascontiguousarray(scaled.reshape(k // 512, 128, 4, n).transpose(0, 1, 3, 2))
    if fmt == "e4m3":
        words = by_word.astype(ml_dtypes.float8_e4m3fn).view(np.uint8)
    else:
        c = by_word.astype(ml_dtypes.float4_e2m1fn).view(np.uint8) & 0xF
        words = c[..., 0::2] | (c[..., 1::2] << 4)
    return np.ascontiguousarray(words), np.ascontiguousarray(byte.astype(np.uint8).reshape(k // 512, 16, n))


def unpack_weight(words, scales, fmt):
    g, p, n, _ = words.shape
    if fmt == "e4m3":
        vals = np.ascontiguousarray(words).view(ml_dtypes.float8_e4m3fn).astype(np.float64)
    else:
        nib = np.empty((g, p, n, 4), np.uint8)
        nib[..., 0::2] = words & 0xF
        nib[..., 1::2] = words >> 4
        vals = E2M1[nib]
    vals = vals * np.repeat(np.exp2(scales.astype(np.float64) - 127.0), 8, axis=1)[..., None]
    return vals.transpose(0, 1, 3, 2).reshape(g * 512, n)

def pack4(w):
    words, scales = pack_weight(w, "e2m1")
    return words.reshape(words.shape[0], 128, -1), scales


def unpack4(words, scales):
    return unpack_weight(words.reshape(words.shape[0], 128, -1, 2), scales, "e2m1")


B, S, D, E, HD = 2, 512, 512, 512, 64
ROPE_BASE = 10000.0


def rope_tables():
    inv_freq = 1.0 / ROPE_BASE ** (np.arange(0, E, 2) / E)
    ang = np.repeat(np.arange(S)[:, None] * inv_freq[None, :], 2, axis=-1)
    return np.cos(ang), np.sin(ang)


def rotate_half(v):
    h = v.shape[-1] // 2
    return np.concatenate([-v[..., h:], v[..., :h]], axis=-1)


def setup_inputs():
    s = mx_kscale(D)
    x = bf(np.random.standard_normal((B, S, D)) * s)
    Wq_words, Wq_scales = pack4(np.random.standard_normal((D, E)) * 0.5 / np.sqrt(D) / s[:, None])
    bq = bf(np.random.standard_normal(E) * 0.1)
    Wk_words, Wk_scales = pack4(np.random.standard_normal((D, E)) * 0.5 / np.sqrt(D) / s[:, None])
    bk = bf(np.random.standard_normal(E) * 0.1)
    return {"x": x,
            "Wq_words": Wq_words,
            "Wq_scales": Wq_scales,
            "bq": bq,
            "Wk_words": Wk_words,
            "Wk_scales": Wk_scales,
            "bk": bk}


def reference(x, Wq_words, Wq_scales, bq, Wk_words, Wk_scales, bk):
    xq = mxq(f64(x), 2, "e4m3")
    q = (xq @ unpack4(Wq_words, Wq_scales)) + f64(bq)
    k = (xq @ unpack4(Wk_words, Wk_scales)) + f64(bk)
    cos, sin = rope_tables()
    qr = q * cos + rotate_half(q) * sin
    kr = k * cos + rotate_half(k) * sin
    return qr, kr

@@ -1,0 +1,228 @@
+import math
+from contextlib import ExitStack
+
+import concourse.mybir as mybir
+from concourse.masks import make_identity
+
+F32 = mybir.dt.float32
+BF16 = mybir.dt.bfloat16
+I32 = mybir.dt.int32
+U32 = mybir.dt.uint32
+U8 = mybir.dt.uint8
+FP8X4 = mybir.dt.float8_e4m3fn_x4
+FP4X4 = mybir.dt.float4_e2m1fn_x4
+ALU = mybir.AluOpType
+ACT = mybir.ActivationFunctionType
+
+P = 128
+BATCH = 2
+SEQ = 512
+DIM = 512
+FEAT = 512
+ROPE_BASE = 10000.0
+PACK = 4
+F_TILES = FEAT // P
+T_TILES = SEQ // P
+HALF_TILES = F_TILES // 2
+TWO_PI = 2.0 * math.pi
+
+FLOPS = 2 * BATCH * SEQ * DIM * 2 * FEAT
+
+
+def tile_ropemultiheadattention_pa_kernel(
+    tc, x, Wq_words, Wq_scales, bq, Wk_words, Wk_scales, bk, out_0, out_1
+):
+    nc = tc.nc
+    weights = ((Wq_words, Wq_scales, bq, out_0), (Wk_words, Wk_scales, bk, out_1))
+
+    with ExitStack() as ctx:
+        keep = ctx.enter_context(tc.tile_pool(name="keep", bufs=1))
+        work = ctx.enter_context(tc.tile_pool(name="work", bufs=2))
+        parts = ctx.enter_context(tc.tile_pool(name="parts", bufs=4))
+        psum_mx = ctx.enter_context(tc.psum_pool(name="psum_mx", bufs=4))
+        psum_tr = ctx.enter_context(tc.psum_pool(name="psum_tr", bufs=4))
+
+        x_sb = []
+        for b in range(BATCH):
+            x_sb.append(keep.tile([P, T_TILES, DIM], BF16, name="x_sb%d" % b))
+        x_rows = [x[b].rearrange("(n t) k -> n t k", t=T_TILES) for b in range(BATCH)]
+
+        def load_x(b):
+            for half in range(2):
+                ts = slice(2 * half, 2 * half + 2)
+                nc.sync.dma_start(out=x_sb[b][:, ts, :], in_=x_rows[b][:, ts, :])
+
+        w_words = keep.tile([P, 2, 2 * FEAT], U8, align_bytes=64)
+        w_planes = keep.tile([P, 2, FEAT], U8, align_bytes=64)
+        nc.vector.memset(w_planes[:].rearrange("p w n -> p (w n)").bitcast(I32), 0)
+
+        def load_weight(w):
+            words, scales = weights[w][0], weights[w][1]
+            nc.sync.dma_start(out=w_words[:, w, :].bitcast(I32), in_=words[0].bitcast(I32))
+            for quad in range(4):
+                nc.sync.dma_start(
+                    out=w_planes[32 * quad : 32 * quad + 4, w, :].bitcast(I32),
+                    in_=scales[0, 4 * quad : 4 * quad + 4, :].bitcast(I32),
+                )
+
+        load_x(0)
+        load_weight(0)
+        load_weight(1)
+        load_x(1)
+
+        bias = keep.tile([P, 2 * F_TILES], F32)
+        with nc.allow_non_contiguous_dma(reason="1 KiB of bias, one element a partition"):
+            for w in range(2):
+                bias_bf = keep.tile([P, F_TILES], BF16, name="bias_bf%d" % w)
+                nc.scalar.dma_start(
+                    out=bias_bf[:], in_=weights[w][2].rearrange("(f p) -> p f", p=P)
+                )
+                nc.vector.tensor_copy(
+                    out=bias[:, F_TILES * w : F_TILES * (w + 1)], in_=bias_bf[:]
+                )
+
+        ident = keep.tile([P, P], F32)
+        make_identity(nc, ident[:])
+
+        pos = keep.tile([P, SEQ], F32)
+        nc.gpsimd.iota(
+            pos[:],
+            pattern=[[1, T_TILES], [T_TILES, P]],
+            base=0,
+            channel_multiplier=0,
+            allow_small_or_imprecise_dtypes=True,
+        )
+
+        freq_row = keep.tile([P, P], F32)
+        nc.vector.memset(freq_row[:, 0:2], 1.0)
+        nc.vector.tensor_scalar_mul(
+            out=freq_row[:, 0:2], in0=freq_row[:, 0:2], scalar1=1.0 / TWO_PI
+        )
+        for width in (2, 8, 32):
+            for m in range(1, 4):
+                nc.vector.tensor_scalar_mul(
+                    out=freq_row[:, m * width : (m + 1) * width],
+                    in0=freq_row[:, 0:width],
+                    scalar1=ROPE_BASE ** (-(m * width) / FEAT),
+                )
+        freq_col = psum_tr.tile([P, T_TILES, P], F32, tag="tr")
+        nc.tensor.transpose(freq_col[:, 0, :], freq_row[:], ident[:])
+        turns = keep.tile([P, F_TILES], F32)
+        for f in range(F_TILES):
+            nc.vector.tensor_scalar_mul(
+                out=turns[:, f : f + 1],
+                in0=freq_col[:, 0, 0:1],
+                scalar1=ROPE_BASE ** (-(f * P) / FEAT),
+            )
+
+        cos_tab = keep.tile([P, F_TILES, SEQ], F32)
+        sin_tab = keep.tile([P, F_TILES, SEQ], F32)
+
+        def make_tables(f):
+            whole = work.tile([P, SEQ], I32)
+            nc.vector.tensor_scalar(
+                out=whole[:], in0=pos[:], scalar1=turns[:, f : f + 1], scalar2=None,
+                op0=ALU.mult,
+            )
+            frac = work.tile([P, SEQ], F32)
+            nc.vector.scalar_tensor_tensor(
+                out=frac[:], in0=pos[:], scalar=turns[:, f : f + 1], in1=whole[:],
+                op0=ALU.mult, op1=ALU.subtract,
+            )
+            sign = -1.0 if f < HALF_TILES else 1.0
+            nc.scalar.activation(
+                out=sin_tab[:, f, :], in_=frac[:], func=ACT.Sin, scale=sign * TWO_PI
+            )
+            dist = work.tile([P, SEQ], F32)
+            nc.scalar.activation(out=dist[:], in_=frac[:], func=ACT.Abs)
+            nc.scalar.activation(
+                out=cos_tab[:, f, :], in_=dist[:], func=ACT.Sin, scale=-TWO_PI,
+                bias=math.pi / 2.0,
+            )
+
+        x_codes = keep.tile([P, BATCH, SEQ], U32, align_bytes=64)
+        x_planes = keep.tile([P, BATCH, SEQ], U8, align_bytes=64)
+
+        def quantise_x(b):
+            x_words = x_sb[b][:].rearrange("p t k -> p (t k)").bitcast(F32)
+            grouped = keep.tile([P, SEQ, PACK], BF16, align_bytes=64, name="grouped%d" % b)
+            grouped_words = (
+                grouped[:].rearrange("p c t -> p (c t)").bitcast(F32)
+                .rearrange("p (h t n u) -> p h t n u", h=2, t=2, u=2)
+            )
+            for half in range(2):
+                flipped = psum_tr.tile([P, T_TILES, P], F32, tag="tr")
+                for tl in range(2):
+                    first = (DIM // 2) * (2 * half + tl)
+                    for u in range(2):
+                        nc.tensor.transpose(
+                            flipped[:, 2 * tl + u, :],
+                            x_words[:, first + u : first + DIM // 2 : 2],
+                            ident[:],
+                        )
+                pairs = flipped[:].rearrange("p (t u) n -> p t n u", u=2)
+                if half == 0:
+                    nc.vector.tensor_copy(out=grouped_words[:, half], in_=pairs)
+                else:
+                    nc.scalar.copy(out=grouped_words[:, half], in_=pairs)
+            nc.vector.quantize_mx(
+                out=x_codes[:, b, :].bitcast(FP8X4),
+                scales=x_planes[:, b, :],
+                in_=grouped[:].rearrange("p c t -> p (c t)"),
+            )
+
+        def project(b, w, f):
+            acc = psum_mx.tile([P, SEQ], F32, tag="acc")
+            nc.tensor.matmul_mx(
+                out=acc[:],
+                lhsT=w_words[:, w, 2 * P * f : 2 * P * (f + 1)].bitcast(FP4X4),
+                lhsT_scale=w_planes[:, w, P * f : P * (f + 1)],
+                rhs=x_codes[:, b, :].bitcast(FP8X4),
+                rhs_scale=x_planes[:, b, :],
+                start=True,
+                stop=True,
+            )
+            return acc
+
+        def rotate_and_store(b, w, f, own, other):
+            f_other = (f + HALF_TILES) % F_TILES
+            part_cos = parts.tile([P, SEQ], F32)
+            nc.vector.scalar_tensor_tensor(
+                out=part_cos[:], in0=own[:], scalar=bias[:, F_TILES * w + f : F_TILES * w + f + 1],
+                in1=cos_tab[:, f, :], op0=ALU.add, op1=ALU.mult,
+            )
+            part_sin = parts.tile([P, SEQ], F32)
+            nc.vector.scalar_tensor_tensor(
+                out=part_sin[:], in0=other[:],
+                scalar=bias[:, F_TILES * w + f_other : F_TILES * w + f_other + 1],
+                in1=sin_tab[:, f, :], op0=ALU.add, op1=ALU.mult,
+            )
+            back = psum_tr.tile([P, T_TILES, P], F32, tag="tr")
+            for t in range(T_TILES):
+                cols = slice(P * t, P * (t + 1))
+                nc.tensor.matmul(
+                    out=back[:, t, :], lhsT=part_cos[:, cols], rhs=ident[:],
+                    is_transpose=True, start=True, stop=False,
+                )
+                nc.tensor.matmul(
+                    out=back[:, t, :], lhsT=part_sin[:, cols], rhs=ident[:],
+                    is_transpose=True, start=False, stop=True,
+                )
+            rows = parts.tile([P, T_TILES, P], F32)
+            nc.scalar.copy(out=rows[:], in_=back[:])
+            out_rows = weights[w][3][b].rearrange("(n t) i -> n t i", t=T_TILES)
+            nc.sync.dma_start(out=out_rows[:, :, P * f : P * (f + 1)], in_=rows[:])
+
+        make_tables(0)
+        make_tables(HALF_TILES)
+        quantise_x(0)
+        make_tables(1)
+        make_tables(1 + HALF_TILES)
+        quantise_x(1)
+        for b in range(BATCH):
+            for f in range(HALF_TILES):
+                for w in range(2):
+                    low = project(b, w, f)
+                    high = project(b, w, f + HALF_TILES)
+                    rotate_and_store(b, w, f, low, high)
+                    rotate_and_store(b, w, f + HALF_TILES, high, low)

@@ -197,16 +197,14 @@ def tile_ropemultiheadattention_pa_kernel(
                 scalar=bias[:, F_TILES * w + f_other : F_TILES * w + f_other + 1],
                 in1=sin_tab[:, f, :], op0=ALU.add, op1=ALU.mult,
             )
+            rotated = parts.tile([P, SEQ], F32)
+            nc.gpsimd.tensor_tensor(
+                out=rotated[:], in0=part_cos[:], in1=part_sin[:], op=ALU.add
+            )
             back = psum_tr.tile([P, T_TILES, P], F32, tag="tr")
             for t in range(T_TILES):
-                cols = slice(P * t, P * (t + 1))
-                nc.tensor.matmul(
-                    out=back[:, t, :], lhsT=part_cos[:, cols], rhs=ident[:],
-                    is_transpose=True, start=True, stop=False,
-                )
-                nc.tensor.matmul(
-                    out=back[:, t, :], lhsT=part_sin[:, cols], rhs=ident[:],
-                    is_transpose=True, start=False, stop=True,
+                nc.tensor.transpose(
+                    back[:, t, :], rotated[:, P * t : P * (t + 1)], ident[:]
                 )
             rows = parts.tile([P, T_TILES, P], F32)
             nc.scalar.copy(out=rows[:], in_=back[:])

@@ -25,6 +25,7 @@ F_TILES = FEAT // P
 T_TILES = SEQ // P
 HALF_TILES = F_TILES // 2
 TWO_PI = 2.0 * math.pi
+GPSIMD_TILES = 3
 
 FLOPS = 2 * BATCH * SEQ * DIM * 2 * FEAT
 
@@ -36,25 +37,38 @@ def tile_ropemultiheadattention_pa_kernel(
     weights = ((Wq_words, Wq_scales, bq, out_0), (Wk_words, Wk_scales, bk, out_1))
 
     with ExitStack() as ctx:
+        ctx.enter_context(tc.manual_schedule())
         keep = ctx.enter_context(tc.tile_pool(name="keep", bufs=1))
-        work = ctx.enter_context(tc.tile_pool(name="work", bufs=2))
-        parts = ctx.enter_context(tc.tile_pool(name="parts", bufs=4))
+        parts = ctx.enter_context(tc.tile_pool(name="parts", bufs=6))
         psum_mx = ctx.enter_context(tc.psum_pool(name="psum_mx", bufs=4))
         psum_tr = ctx.enter_context(tc.psum_pool(name="psum_tr", bufs=4))
 
-        x_sb = []
-        for b in range(BATCH):
-            x_sb.append(keep.tile([P, T_TILES, DIM], BF16, name="x_sb%d" % b))
-        x_rows = [x[b].rearrange("(n t) k -> n t k", t=T_TILES) for b in range(BATCH)]
-
-        def load_x(b):
-            for half in range(2):
-                ts = slice(2 * half, 2 * half + 2)
-                nc.sync.dma_start(out=x_sb[b][:, ts, :], in_=x_rows[b][:, ts, :])
-
+        x_sb = [keep.tile([P, T_TILES, DIM], BF16, name="x_sb%d" % b) for b in range(BATCH)]
+        grouped = [
+            keep.tile([P, SEQ, PACK], BF16, align_bytes=64, name="grouped%d" % b)
+            for b in range(BATCH)
+        ]
+        x_codes = keep.tile([P, BATCH, SEQ], U32, align_bytes=64)
+        x_planes = keep.tile([P, BATCH, SEQ], U8, align_bytes=64)
         w_words = keep.tile([P, 2, 2 * FEAT], U8, align_bytes=64)
         w_planes = keep.tile([P, 2, FEAT], U8, align_bytes=64)
-        nc.vector.memset(w_planes[:].rearrange("p w n -> p (w n)").bitcast(I32), 0)
+        bias_bf = [keep.tile([P, F_TILES], BF16, name="bias_bf%d" % w) for w in range(2)]
+        bias = keep.tile([P, 2 * F_TILES], F32)
+        ident = keep.tile([P, P], F32)
+        pos = keep.tile([P, SEQ], F32)
+        freq_row = keep.tile([P, P], F32)
+        turns = keep.tile([P, F_TILES], F32)
+        whole = keep.tile([P, F_TILES, SEQ], I32)
+        frac = keep.tile([P, F_TILES, SEQ], F32)
+        dist = keep.tile([P, F_TILES, SEQ], F32)
+        cos_tab = keep.tile([P, F_TILES, SEQ], F32)
+        sin_tab = keep.tile([P, F_TILES, SEQ], F32)
+
+        def load_x(b):
+            x_rows = x[b].rearrange("(n t) k -> n t k", t=T_TILES)
+            for half in range(2):
+                ts = slice(2 * half, 2 * half + 2)
+                nc.sync.dma_start(out=x_sb[b][:, ts, :], in_=x_rows[:, ts, :])
 
         def load_weight(w):
             words, scales = weights[w][0], weights[w][1]
@@ -65,26 +79,18 @@ def tile_ropemultiheadattention_pa_kernel(
                     in_=scales[0, 4 * quad : 4 * quad + 4, :].bitcast(I32),
                 )
 
+        nc.vector.memset(w_planes[:].rearrange("p w n -> p (w n)").bitcast(I32), 0)
         load_x(0)
         load_weight(0)
-        load_weight(1)
         load_x(1)
-
-        bias = keep.tile([P, 2 * F_TILES], F32)
+        load_weight(1)
         with nc.allow_non_contiguous_dma(reason="1 KiB of bias, one element a partition"):
             for w in range(2):
-                bias_bf = keep.tile([P, F_TILES], BF16, name="bias_bf%d" % w)
                 nc.scalar.dma_start(
-                    out=bias_bf[:], in_=weights[w][2].rearrange("(f p) -> p f", p=P)
-                )
-                nc.vector.tensor_copy(
-                    out=bias[:, F_TILES * w : F_TILES * (w + 1)], in_=bias_bf[:]
+                    out=bias_bf[w][:], in_=weights[w][2].rearrange("(f p) -> p f", p=P)
                 )
 
-        ident = keep.tile([P, P], F32)
         make_identity(nc, ident[:])
-
-        pos = keep.tile([P, SEQ], F32)
         nc.gpsimd.iota(
             pos[:],
             pattern=[[1, T_TILES], [T_TILES, P]],
@@ -92,8 +98,6 @@ def tile_ropemultiheadattention_pa_kernel(
             channel_multiplier=0,
             allow_small_or_imprecise_dtypes=True,
         )
-
-        freq_row = keep.tile([P, P], F32)
         nc.vector.memset(freq_row[:, 0:2], 1.0)
         nc.vector.tensor_scalar_mul(
             out=freq_row[:, 0:2], in0=freq_row[:, 0:2], scalar1=1.0 / TWO_PI
@@ -107,7 +111,6 @@ def tile_ropemultiheadattention_pa_kernel(
                 )
         freq_col = psum_tr.tile([P, T_TILES, P], F32, tag="tr")
         nc.tensor.transpose(freq_col[:, 0, :], freq_row[:], ident[:])
-        turns = keep.tile([P, F_TILES], F32)
         for f in range(F_TILES):
             nc.vector.tensor_scalar_mul(
                 out=turns[:, f : f + 1],
@@ -115,80 +118,86 @@ def tile_ropemultiheadattention_pa_kernel(
                 scalar1=ROPE_BASE ** (-(f * P) / FEAT),
             )
 
-        cos_tab = keep.tile([P, F_TILES, SEQ], F32)
-        sin_tab = keep.tile([P, F_TILES, SEQ], F32)
-
-        def make_tables(f):
-            whole = work.tile([P, SEQ], I32)
-            nc.vector.tensor_scalar(
-                out=whole[:], in0=pos[:], scalar1=turns[:, f : f + 1], scalar2=None,
-                op0=ALU.mult,
+        def round_turns(f):
+            nc.gpsimd.tensor_scalar(
+                out=whole[:, f, :], in0=pos[:], scalar1=turns[:, f : f + 1], scalar2=0.0,
+                op0=ALU.mult, op1=ALU.add,
             )
-            frac = work.tile([P, SEQ], F32)
+
+        def reduce_turns(f):
             nc.vector.scalar_tensor_tensor(
-                out=frac[:], in0=pos[:], scalar=turns[:, f : f + 1], in1=whole[:],
+                out=frac[:, f, :], in0=pos[:], scalar=turns[:, f : f + 1], in1=whole[:, f, :],
                 op0=ALU.mult, op1=ALU.subtract,
             )
+
+        def sin_and_cos(f):
             sign = -1.0 if f < HALF_TILES else 1.0
             nc.scalar.activation(
-                out=sin_tab[:, f, :], in_=frac[:], func=ACT.Sin, scale=sign * TWO_PI
+                out=sin_tab[:, f, :], in_=frac[:, f, :], func=ACT.Sin, scale=sign * TWO_PI
             )
-            dist = work.tile([P, SEQ], F32)
-            nc.scalar.activation(out=dist[:], in_=frac[:], func=ACT.Abs)
+            nc.scalar.activation(out=dist[:, f, :], in_=frac[:, f, :], func=ACT.Abs)
             nc.scalar.activation(
-                out=cos_tab[:, f, :], in_=dist[:], func=ACT.Sin, scale=-TWO_PI,
+                out=cos_tab[:, f, :], in_=dist[:, f, :], func=ACT.Sin, scale=-TWO_PI,
                 bias=math.pi / 2.0,
             )
 
-        x_codes = keep.tile([P, BATCH, SEQ], U32, align_bytes=64)
-        x_planes = keep.tile([P, BATCH, SEQ], U8, align_bytes=64)
-
-        def quantise_x(b):
+        def flip_x(b, half):
             x_words = x_sb[b][:].rearrange("p t k -> p (t k)").bitcast(F32)
-            grouped = keep.tile([P, SEQ, PACK], BF16, align_bytes=64, name="grouped%d" % b)
+            flipped = psum_tr.tile([P, T_TILES, P], F32, tag="tr")
+            for tl in range(2):
+                first = (DIM // 2) * (2 * half + tl)
+                for u in range(2):
+                    nc.tensor.transpose(
+                        flipped[:, 2 * tl + u, :],
+                        x_words[:, first + u : first + DIM // 2 : 2],
+                        ident[:],
+                    )
+            return flipped
+
+        def group_x(copy, b, half, flipped):
             grouped_words = (
-                grouped[:].rearrange("p c t -> p (c t)").bitcast(F32)
+                grouped[b][:].rearrange("p c t -> p (c t)").bitcast(F32)
                 .rearrange("p (h t n u) -> p h t n u", h=2, t=2, u=2)
             )
-            for half in range(2):
-                flipped = psum_tr.tile([P, T_TILES, P], F32, tag="tr")
-                for tl in range(2):
-                    first = (DIM // 2) * (2 * half + tl)
-                    for u in range(2):
-                        nc.tensor.transpose(
-                            flipped[:, 2 * tl + u, :],
-                            x_words[:, first + u : first + DIM // 2 : 2],
-                            ident[:],
-                        )
-                pairs = flipped[:].rearrange("p (t u) n -> p t n u", u=2)
-                if half == 0:
-                    nc.vector.tensor_copy(out=grouped_words[:, half], in_=pairs)
-                else:
-                    nc.scalar.copy(out=grouped_words[:, half], in_=pairs)
+            copy(
+                out=grouped_words[:, half],
+                in_=flipped[:].rearrange("p (t u) n -> p t n u", u=2),
+            )
+
+        def quantise_x(b):
             nc.vector.quantize_mx(
                 out=x_codes[:, b, :].bitcast(FP8X4),
                 scales=x_planes[:, b, :],
-                in_=grouped[:].rearrange("p c t -> p (c t)"),
+                in_=grouped[b][:].rearrange("p c t -> p (c t)"),
             )
 
-        def project(b, w, f):
-            acc = psum_mx.tile([P, SEQ], F32, tag="acc")
-            nc.tensor.matmul_mx(
-                out=acc[:],
-                lhsT=w_words[:, w, 2 * P * f : 2 * P * (f + 1)].bitcast(FP4X4),
-                lhsT_scale=w_planes[:, w, P * f : P * (f + 1)],
-                rhs=x_codes[:, b, :].bitcast(FP8X4),
-                rhs_scale=x_planes[:, b, :],
-                start=True,
-                stop=True,
-            )
-            return acc
+        steps = [
+            (b, w, f) for b in range(BATCH) for f in range(HALF_TILES) for w in range(2)
+        ]
 
-        def rotate_and_store(b, w, f, own, other):
+        def project(step):
+            b, w, f_low = step
+            banks = []
+            for f in (f_low, f_low + HALF_TILES):
+                acc = psum_mx.tile([P, SEQ], F32, tag="acc")
+                nc.tensor.matmul_mx(
+                    out=acc[:],
+                    lhsT=w_words[:, w, 2 * P * f : 2 * P * (f + 1)].bitcast(FP4X4),
+                    lhsT_scale=w_planes[:, w, P * f : P * (f + 1)],
+                    rhs=x_codes[:, b, :].bitcast(FP8X4),
+                    rhs_scale=x_planes[:, b, :],
+                    start=True,
+                    stop=True,
+                )
+                banks.append(acc)
+            return banks
+
+        def rotate(w, f, own, other):
             f_other = (f + HALF_TILES) % F_TILES
             part_cos = parts.tile([P, SEQ], F32)
             nc.vector.scalar_tensor_tensor(
-                out=part_cos[:], in0=own[:], scalar=bias[:, F_TILES * w + f : F_TILES * w + f + 1],
+                out=part_cos[:], in0=own[:],
+                scalar=bias[:, F_TILES * w + f : F_TILES * w + f + 1],
                 in1=cos_tab[:, f, :], op0=ALU.add, op1=ALU.mult,
             )
             part_sin = parts.tile([P, SEQ], F32)
@@ -197,30 +206,63 @@ def tile_ropemultiheadattention_pa_kernel(
                 scalar=bias[:, F_TILES * w + f_other : F_TILES * w + f_other + 1],
                 in1=sin_tab[:, f, :], op0=ALU.add, op1=ALU.mult,
             )
-            rotated = parts.tile([P, SEQ], F32)
+            summed = parts.tile([P, GPSIMD_TILES * P], F32)
             nc.gpsimd.tensor_tensor(
-                out=rotated[:], in0=part_cos[:], in1=part_sin[:], op=ALU.add
+                out=summed[:], in0=part_cos[:, 0 : GPSIMD_TILES * P],
+                in1=part_sin[:, 0 : GPSIMD_TILES * P], op=ALU.add,
             )
+            return part_cos, part_sin, summed
+
+        def turn_back_and_store(b, w, f, part_cos, part_sin, summed):
             back = psum_tr.tile([P, T_TILES, P], F32, tag="tr")
-            for t in range(T_TILES):
-                nc.tensor.transpose(
-                    back[:, t, :], rotated[:, P * t : P * (t + 1)], ident[:]
+            for t in range(GPSIMD_TILES, T_TILES):
+                cols = slice(P * t, P * (t + 1))
+                nc.tensor.matmul(
+                    out=back[:, t, :], lhsT=part_cos[:, cols], rhs=ident[:],
+                    is_transpose=True, start=True, stop=False,
                 )
+                nc.tensor.matmul(
+                    out=back[:, t, :], lhsT=part_sin[:, cols], rhs=ident[:],
+                    is_transpose=True, start=False, stop=True,
+                )
+            for t in range(GPSIMD_TILES):
+                nc.tensor.transpose(back[:, t, :], summed[:, P * t : P * (t + 1)], ident[:])
             rows = parts.tile([P, T_TILES, P], F32)
             nc.scalar.copy(out=rows[:], in_=back[:])
             out_rows = weights[w][3][b].rearrange("(n t) i -> n t i", t=T_TILES)
             nc.sync.dma_start(out=out_rows[:, :, P * f : P * (f + 1)], in_=rows[:])
 
-        make_tables(0)
-        make_tables(HALF_TILES)
+        for f in (0, 2, 1, 3):
+            round_turns(f)
+        reduce_turns(0)
+        sin_and_cos(0)
+        reduce_turns(2)
+        reduce_turns(1)
+        flipped_0 = [flip_x(0, half) for half in range(2)]
+        group_x(nc.vector.tensor_copy, 0, 0, flipped_0[0])
+        group_x(nc.scalar.copy, 0, 1, flipped_0[1])
+        sin_and_cos(2)
         quantise_x(0)
-        make_tables(1)
-        make_tables(1 + HALF_TILES)
-        quantise_x(1)
-        for b in range(BATCH):
-            for f in range(HALF_TILES):
-                for w in range(2):
-                    low = project(b, w, f)
-                    high = project(b, w, f + HALF_TILES)
-                    rotate_and_store(b, w, f, low, high)
-                    rotate_and_store(b, w, f + HALF_TILES, high, low)
+        reduce_turns(3)
+        for w in range(2):
+            nc.vector.tensor_copy(out=bias[:, F_TILES * w : F_TILES * (w + 1)], in_=bias_bf[w][:])
+        flipped_1 = [flip_x(1, half) for half in range(2)]
+        for half in range(2):
+            group_x(nc.scalar.copy, 1, half, flipped_1[half])
+        sin_and_cos(1)
+        sin_and_cos(3)
+
+        banks = {0: project(steps[0]), 1: project(steps[1])}
+        for s in range(len(steps)):
+            b, w, f_low = steps[s]
+            f_high = f_low + HALF_TILES
+            low, high = banks[s]
+            done_low = rotate(w, f_low, low, high)
+            done_high = rotate(w, f_high, high, low)
+            if s + 2 < len(steps):
+                ahead = steps[s + 2]
+                if ahead[1:] == (0, 0):
+                    quantise_x(ahead[0])
+                banks[s + 2] = project(ahead)
+            turn_back_and_store(b, w, f_low, *done_low)
+            turn_back_and_store(b, w, f_high, *done_high)

@@ -52,8 +52,7 @@ def tile_ropemultiheadattention_pa_kernel(
         x_planes = keep.tile([P, BATCH, SEQ], U8, align_bytes=64)
         w_words = keep.tile([P, 2, 2 * FEAT], U8, align_bytes=64)
         w_planes = keep.tile([P, 2, FEAT], U8, align_bytes=64)
-        bias_bf = [keep.tile([P, F_TILES], BF16, name="bias_bf%d" % w) for w in range(2)]
-        bias = keep.tile([P, 2 * F_TILES], F32)
+        bias = [keep.tile([P, F_TILES], BF16, name="bias%d" % w) for w in range(2)]
         ident = keep.tile([P, P], F32)
         pos = keep.tile([P, SEQ], F32)
         freq_row = keep.tile([P, P], F32)
@@ -79,7 +78,7 @@ def tile_ropemultiheadattention_pa_kernel(
                     in_=scales[0, 4 * quad : 4 * quad + 4, :].bitcast(I32),
                 )
 
-        nc.vector.memset(w_planes[:].rearrange("p w n -> p (w n)").bitcast(I32), 0)
+        nc.gpsimd.memset(w_planes[:].rearrange("p w n -> p (w n)").bitcast(F32), 0.0)
         load_x(0)
         load_weight(0)
         load_x(1)
@@ -87,7 +86,7 @@ def tile_ropemultiheadattention_pa_kernel(
         with nc.allow_non_contiguous_dma(reason="1 KiB of bias, one element a partition"):
             for w in range(2):
                 nc.scalar.dma_start(
-                    out=bias_bf[w][:], in_=weights[w][2].rearrange("(f p) -> p f", p=P)
+                    out=bias[w][:], in_=weights[w][2].rearrange("(f p) -> p f", p=P)
                 )
 
         make_identity(nc, ident[:])
@@ -99,9 +98,6 @@ def tile_ropemultiheadattention_pa_kernel(
             allow_small_or_imprecise_dtypes=True,
         )
         nc.vector.memset(freq_row[:, 0:2], 1.0)
-        nc.vector.tensor_scalar_mul(
-            out=freq_row[:, 0:2], in0=freq_row[:, 0:2], scalar1=1.0 / TWO_PI
-        )
         for width in (2, 8, 32):
             for m in range(1, 4):
                 nc.vector.tensor_scalar_mul(
@@ -115,11 +111,11 @@ def tile_ropemultiheadattention_pa_kernel(
             nc.vector.tensor_scalar_mul(
                 out=turns[:, f : f + 1],
                 in0=freq_col[:, 0, 0:1],
-                scalar1=ROPE_BASE ** (-(f * P) / FEAT),
+                scalar1=ROPE_BASE ** (-(f * P) / FEAT) / TWO_PI,
             )
 
-        def round_turns(f):
-            nc.gpsimd.tensor_scalar(
+        def round_turns(engine, f):
+            engine.tensor_scalar(
                 out=whole[:, f, :], in0=pos[:], scalar1=turns[:, f : f + 1], scalar2=0.0,
                 op0=ALU.mult, op1=ALU.add,
             )
@@ -164,11 +160,12 @@ def tile_ropemultiheadattention_pa_kernel(
                 in_=flipped[:].rearrange("p (t u) n -> p t n u", u=2),
             )
 
-        def quantise_x(b):
+        def quantise_x(b, half):
+            cols = slice((SEQ // 2) * half, (SEQ // 2) * (half + 1))
             nc.vector.quantize_mx(
-                out=x_codes[:, b, :].bitcast(FP8X4),
-                scales=x_planes[:, b, :],
-                in_=grouped[b][:].rearrange("p c t -> p (c t)"),
+                out=x_codes[:, b, cols].bitcast(FP8X4),
+                scales=x_planes[:, b, cols],
+                in_=grouped[b][:, cols, :].rearrange("p c t -> p (c t)"),
             )
 
         steps = [
@@ -192,22 +189,22 @@ def tile_ropemultiheadattention_pa_kernel(
                 banks.append(acc)
             return banks
 
-        def rotate(w, f, own, other):
+        def rotate(adder, w, f, own, other):
             f_other = (f + HALF_TILES) % F_TILES
             part_cos = parts.tile([P, SEQ], F32)
             nc.vector.scalar_tensor_tensor(
                 out=part_cos[:], in0=own[:],
-                scalar=bias[:, F_TILES * w + f : F_TILES * w + f + 1],
+                scalar=bias[w][:, f : f + 1],
                 in1=cos_tab[:, f, :], op0=ALU.add, op1=ALU.mult,
             )
             part_sin = parts.tile([P, SEQ], F32)
             nc.vector.scalar_tensor_tensor(
                 out=part_sin[:], in0=other[:],
-                scalar=bias[:, F_TILES * w + f_other : F_TILES * w + f_other + 1],
+                scalar=bias[w][:, f_other : f_other + 1],
                 in1=sin_tab[:, f, :], op0=ALU.add, op1=ALU.mult,
             )
             summed = parts.tile([P, GPSIMD_TILES * P], F32)
-            nc.gpsimd.tensor_tensor(
+            adder.tensor_tensor(
                 out=summed[:], in0=part_cos[:, 0 : GPSIMD_TILES * P],
                 in1=part_sin[:, 0 : GPSIMD_TILES * P], op=ALU.add,
             )
@@ -232,20 +229,19 @@ def tile_ropemultiheadattention_pa_kernel(
             out_rows = weights[w][3][b].rearrange("(n t) i -> n t i", t=T_TILES)
             nc.sync.dma_start(out=out_rows[:, :, P * f : P * (f + 1)], in_=rows[:])
 
-        for f in (0, 2, 1, 3):
-            round_turns(f)
+        round_turns(nc.vector, 0)
+        for f in (2, 1, 3):
+            round_turns(nc.gpsimd, f)
         reduce_turns(0)
         sin_and_cos(0)
-        reduce_turns(2)
-        reduce_turns(1)
+        for f in (2, 1, 3):
+            reduce_turns(f)
         flipped_0 = [flip_x(0, half) for half in range(2)]
         group_x(nc.vector.tensor_copy, 0, 0, flipped_0[0])
+        quantise_x(0, 0)
         group_x(nc.scalar.copy, 0, 1, flipped_0[1])
         sin_and_cos(2)
-        quantise_x(0)
-        reduce_turns(3)
-        for w in range(2):
-            nc.vector.tensor_copy(out=bias[:, F_TILES * w : F_TILES * (w + 1)], in_=bias_bf[w][:])
+        quantise_x(0, 1)
         flipped_1 = [flip_x(1, half) for half in range(2)]
         for half in range(2):
             group_x(nc.scalar.copy, 1, half, flipped_1[half])
@@ -257,12 +253,14 @@ def tile_ropemultiheadattention_pa_kernel(
             b, w, f_low = steps[s]
             f_high = f_low + HALF_TILES
             low, high = banks[s]
-            done_low = rotate(w, f_low, low, high)
-            done_high = rotate(w, f_high, high, low)
+            done_low = rotate(nc.gpsimd, w, f_low, low, high)
+            last_adder = nc.vector if s == len(steps) - 1 else nc.gpsimd
+            done_high = rotate(last_adder, w, f_high, high, low)
             if s + 2 < len(steps):
                 ahead = steps[s + 2]
                 if ahead[1:] == (0, 0):
-                    quantise_x(ahead[0])
+                    quantise_x(ahead[0], 0)
+                    quantise_x(ahead[0], 1)
                 banks[s + 2] = project(ahead)
             turn_back_and_store(b, w, f_low, *done_low)
             turn_back_and_store(b, w, f_high, *done_high)

@@ -80,14 +80,13 @@ def tile_ropemultiheadattention_pa_kernel(
 
         nc.gpsimd.memset(w_planes[:].rearrange("p w n -> p (w n)").bitcast(F32), 0.0)
         load_x(0)
-        load_weight(0)
-        load_x(1)
-        load_weight(1)
         with nc.allow_non_contiguous_dma(reason="1 KiB of bias, one element a partition"):
             for w in range(2):
-                nc.scalar.dma_start(
+                load_weight(w)
+                nc.sync.dma_start(
                     out=bias[w][:], in_=weights[w][2].rearrange("(f p) -> p f", p=P)
                 )
+        load_x(1)
 
         make_identity(nc, ident[:])
         nc.gpsimd.iota(
@@ -236,20 +235,24 @@ def tile_ropemultiheadattention_pa_kernel(
         sin_and_cos(0)
         for f in (2, 1, 3):
             reduce_turns(f)
-        flipped_0 = [flip_x(0, half) for half in range(2)]
-        group_x(nc.vector.tensor_copy, 0, 0, flipped_0[0])
+        flipped = [flip_x(0, half) for half in range(2)]
+        group_x(nc.vector.tensor_copy, 0, 0, flipped[0])
         quantise_x(0, 0)
-        group_x(nc.scalar.copy, 0, 1, flipped_0[1])
-        sin_and_cos(2)
+        group_x(nc.scalar.copy, 0, 1, flipped[1])
         quantise_x(0, 1)
-        flipped_1 = [flip_x(1, half) for half in range(2)]
-        for half in range(2):
-            group_x(nc.scalar.copy, 1, half, flipped_1[half])
-        sin_and_cos(1)
-        sin_and_cos(3)
+        for f in (2, 1, 3):
+            sin_and_cos(f)
+
+        def starts_sequence(s):
+            return s < len(steps) and steps[s][1:] == (0, 0)
 
         banks = {0: project(steps[0]), 1: project(steps[1])}
         for s in range(len(steps)):
+            if starts_sequence(s + 4):
+                flipped = [flip_x(steps[s + 4][0], half) for half in range(2)]
+            if starts_sequence(s + 3):
+                for half in range(2):
+                    group_x(nc.scalar.copy, steps[s + 3][0], half, flipped[half])
             b, w, f_low = steps[s]
             f_high = f_low + HALF_TILES
             low, high = banks[s]
@@ -258,7 +261,7 @@ def tile_ropemultiheadattention_pa_kernel(
             done_high = rotate(last_adder, w, f_high, high, low)
             if s + 2 < len(steps):
                 ahead = steps[s + 2]
-                if ahead[1:] == (0, 0):
+                if starts_sequence(s + 2):
                     quantise_x(ahead[0], 0)
                     quantise_x(ahead[0], 1)
                 banks[s + 2] = project(ahead)

@@ -56,12 +56,16 @@ def tile_ropemultiheadattention_pa_kernel(
         ident = keep.tile([P, P], F32)
         pos = keep.tile([P, SEQ], F32)
         freq_row = keep.tile([P, P], F32)
-        turns = keep.tile([P, F_TILES], F32)
-        whole = keep.tile([P, F_TILES, SEQ], I32)
-        frac = keep.tile([P, F_TILES, SEQ], F32)
+        table_warmer = keep.tile([P, 1], F32)
+        turns = keep.tile([P, HALF_TILES], F32)
+        radians = keep.tile([P, HALF_TILES], F32)
+        minus_radians = keep.tile([P, HALF_TILES], F32)
+        whole = keep.tile([P, HALF_TILES, SEQ], I32)
+        frac = keep.tile([P, HALF_TILES, SEQ], F32)
         dist = keep.tile([P, F_TILES, SEQ], F32)
-        cos_tab = keep.tile([P, F_TILES, SEQ], F32)
-        sin_tab = keep.tile([P, F_TILES, SEQ], F32)
+        from_low = keep.tile([P, HALF_TILES, 2, SEQ], F32)
+        from_high = keep.tile([P, HALF_TILES, 2, SEQ], F32)
+        tables = (from_low, from_high)
 
         def load_x(b):
             x_rows = x[b].rearrange("(n t) k -> n t k", t=T_TILES)
@@ -78,7 +82,9 @@ def tile_ropemultiheadattention_pa_kernel(
                     in_=scales[0, 4 * quad : 4 * quad + 4, :].bitcast(I32),
                 )
 
-        nc.gpsimd.memset(w_planes[:].rearrange("p w n -> p (w n)").bitcast(F32), 0.0)
+        nc.vector.memset(freq_row[:, 0:2], 1.0)
+        nc.scalar.activation(out=table_warmer[:], in_=freq_row[:, 0:1], func=ACT.Sin)
+        nc.vector.memset(w_planes[:].rearrange("p w n -> p (w n)").bitcast(I32), 0)
         load_x(0)
         with nc.allow_non_contiguous_dma(reason="1 KiB of bias, one element a partition"):
             for w in range(2):
@@ -96,7 +102,6 @@ def tile_ropemultiheadattention_pa_kernel(
             channel_multiplier=0,
             allow_small_or_imprecise_dtypes=True,
         )
-        nc.vector.memset(freq_row[:, 0:2], 1.0)
         for width in (2, 8, 32):
             for m in range(1, 4):
                 nc.vector.tensor_scalar_mul(
@@ -106,34 +111,60 @@ def tile_ropemultiheadattention_pa_kernel(
                 )
         freq_col = psum_tr.tile([P, T_TILES, P], F32, tag="tr")
         nc.tensor.transpose(freq_col[:, 0, :], freq_row[:], ident[:])
-        for f in range(F_TILES):
+
+        def per_position(out, f, factor):
             nc.vector.tensor_scalar_mul(
-                out=turns[:, f : f + 1],
-                in0=freq_col[:, 0, 0:1],
-                scalar1=ROPE_BASE ** (-(f * P) / FEAT) / TWO_PI,
+                out=out, in0=freq_col[:, 0, 0:1],
+                scalar1=factor * ROPE_BASE ** (-(f * P) / FEAT),
             )
 
-        def round_turns(engine, f):
+        def round_turns(engine, j):
             engine.tensor_scalar(
-                out=whole[:, f, :], in0=pos[:], scalar1=turns[:, f : f + 1], scalar2=0.0,
+                out=whole[:, j, :], in0=pos[:], scalar1=turns[:, j : j + 1], scalar2=0.0,
                 op0=ALU.mult, op1=ALU.add,
             )
 
-        def reduce_turns(f):
+        def reduce_turns(j):
             nc.vector.scalar_tensor_tensor(
-                out=frac[:, f, :], in0=pos[:], scalar=turns[:, f : f + 1], in1=whole[:, f, :],
+                out=frac[:, j, :], in0=pos[:], scalar=turns[:, j : j + 1], in1=whole[:, j, :],
                 op0=ALU.mult, op1=ALU.subtract,
             )
 
-        def sin_and_cos(f):
-            sign = -1.0 if f < HALF_TILES else 1.0
+        def low_tables(j):
+            nc.scalar.activation(out=dist[:, j, :], in_=frac[:, j, :], func=ACT.Abs)
             nc.scalar.activation(
-                out=sin_tab[:, f, :], in_=frac[:, f, :], func=ACT.Sin, scale=sign * TWO_PI
-            )
-            nc.scalar.activation(out=dist[:, f, :], in_=frac[:, f, :], func=ACT.Abs)
-            nc.scalar.activation(
-                out=cos_tab[:, f, :], in_=dist[:, f, :], func=ACT.Sin, scale=-TWO_PI,
+                out=from_low[:, j, 0, :], in_=dist[:, j, :], func=ACT.Sin, scale=-TWO_PI,
                 bias=math.pi / 2.0,
+            )
+            nc.scalar.activation(
+                out=from_high[:, j, 0, :], in_=frac[:, j, :], func=ACT.Sin, scale=-TWO_PI
+            )
+
+        def highest_tables():
+            nc.scalar.activation(
+                out=from_low[:, 1, 1, :], in_=pos[:], func=ACT.Sin, scale=radians[:, 1:2]
+            )
+            nc.scalar.activation(
+                out=from_high[:, 1, 1, :], in_=pos[:], func=ACT.Sin,
+                scale=minus_radians[:, 1:2], bias=math.pi / 2.0,
+            )
+
+        def third_tables():
+            nc.scalar.activation(
+                out=dist[:, 2, :], in_=pos[:], func=ACT.Abs, scale=radians[:, 0:1],
+                bias=-math.pi / 2.0,
+            )
+            nc.scalar.activation(
+                out=from_low[:, 0, 1, :], in_=dist[:, 2, :], func=ACT.Sin, scale=-1.0,
+                bias=math.pi / 2.0,
+            )
+            nc.scalar.activation(
+                out=dist[:, 3, :], in_=pos[:], func=ACT.Abs, scale=radians[:, 0:1],
+                bias=-math.pi,
+            )
+            nc.scalar.activation(
+                out=from_high[:, 0, 1, :], in_=dist[:, 3, :], func=ACT.Sin, scale=1.0,
+                bias=-math.pi / 2.0,
             )
 
         def flip_x(b, half):
@@ -167,103 +198,122 @@ def tile_ropemultiheadattention_pa_kernel(
                 in_=grouped[b][:, cols, :].rearrange("p c t -> p (c t)"),
             )
 
-        steps = [
-            (b, w, f) for b in range(BATCH) for f in range(HALF_TILES) for w in range(2)
-        ]
+        steps = [(b, w, j) for b in range(BATCH) for j in (1, 0) for w in range(2)]
 
-        def project(step):
-            b, w, f_low = step
+        def project(step, cols=slice(0, SEQ)):
+            b, w, j = step
             banks = []
-            for f in (f_low, f_low + HALF_TILES):
+            for f in (j, j + HALF_TILES):
                 acc = psum_mx.tile([P, SEQ], F32, tag="acc")
                 nc.tensor.matmul_mx(
-                    out=acc[:],
+                    out=acc[:, cols],
                     lhsT=w_words[:, w, 2 * P * f : 2 * P * (f + 1)].bitcast(FP4X4),
                     lhsT_scale=w_planes[:, w, P * f : P * (f + 1)],
-                    rhs=x_codes[:, b, :].bitcast(FP8X4),
-                    rhs_scale=x_planes[:, b, :],
+                    rhs=x_codes[:, b, cols].bitcast(FP8X4),
+                    rhs_scale=x_planes[:, b, cols],
                     start=True,
                     stop=True,
                 )
                 banks.append(acc)
             return banks
 
-        def rotate(adder, w, f, own, other):
-            f_other = (f + HALF_TILES) % F_TILES
-            part_cos = parts.tile([P, SEQ], F32)
+        def multiply(w, j, side, acc, product, first, count, cols=slice(0, SEQ)):
+            f = j + side * HALF_TILES
             nc.vector.scalar_tensor_tensor(
-                out=part_cos[:], in0=own[:],
+                out=product[:, first : first + count, cols],
+                in0=acc[:, cols].unsqueeze(1).to_broadcast([P, count, cols.stop - cols.start]),
                 scalar=bias[w][:, f : f + 1],
-                in1=cos_tab[:, f, :], op0=ALU.add, op1=ALU.mult,
+                in1=tables[side][:, j, first : first + count, cols], op0=ALU.add, op1=ALU.mult,
             )
-            part_sin = parts.tile([P, SEQ], F32)
-            nc.vector.scalar_tensor_tensor(
-                out=part_sin[:], in0=other[:],
-                scalar=bias[w][:, f_other : f_other + 1],
-                in1=sin_tab[:, f, :], op0=ALU.add, op1=ALU.mult,
-            )
-            summed = parts.tile([P, GPSIMD_TILES * P], F32)
-            adder.tensor_tensor(
-                out=summed[:], in0=part_cos[:, 0 : GPSIMD_TILES * P],
-                in1=part_sin[:, 0 : GPSIMD_TILES * P], op=ALU.add,
-            )
-            return part_cos, part_sin, summed
 
-        def turn_back_and_store(b, w, f, part_cos, part_sin, summed):
+        def add_parts(adder, products, summed, first, count):
+            hs = slice(first, first + count)
+            adder.tensor_tensor(
+                out=summed[:, hs, :], in0=products[0][:, hs, 0 : GPSIMD_TILES * P],
+                in1=products[1][:, hs, 0 : GPSIMD_TILES * P], op=ALU.add,
+            )
+
+        def turn_back_and_store(b, w, j, h, products, summed):
+            f = j + h * HALF_TILES
             back = psum_tr.tile([P, T_TILES, P], F32, tag="tr")
             for t in range(GPSIMD_TILES, T_TILES):
                 cols = slice(P * t, P * (t + 1))
                 nc.tensor.matmul(
-                    out=back[:, t, :], lhsT=part_cos[:, cols], rhs=ident[:],
+                    out=back[:, t, :], lhsT=products[0][:, h, cols], rhs=ident[:],
                     is_transpose=True, start=True, stop=False,
                 )
                 nc.tensor.matmul(
-                    out=back[:, t, :], lhsT=part_sin[:, cols], rhs=ident[:],
+                    out=back[:, t, :], lhsT=products[1][:, h, cols], rhs=ident[:],
                     is_transpose=True, start=False, stop=True,
                 )
             for t in range(GPSIMD_TILES):
-                nc.tensor.transpose(back[:, t, :], summed[:, P * t : P * (t + 1)], ident[:])
+                nc.tensor.transpose(back[:, t, :], summed[:, h, P * t : P * (t + 1)], ident[:])
             rows = parts.tile([P, T_TILES, P], F32)
             nc.scalar.copy(out=rows[:], in_=back[:])
             out_rows = weights[w][3][b].rearrange("(n t) i -> n t i", t=T_TILES)
             nc.sync.dma_start(out=out_rows[:, :, P * f : P * (f + 1)], in_=rows[:])
 
-        round_turns(nc.vector, 0)
-        for f in (2, 1, 3):
-            round_turns(nc.gpsimd, f)
-        reduce_turns(0)
-        sin_and_cos(0)
-        for f in (2, 1, 3):
-            reduce_turns(f)
+        per_position(radians[:, 1:2], 3, 1.0)
+        per_position(minus_radians[:, 1:2], 3, -1.0)
+        per_position(turns[:, 1:2], 1, 1.0 / TWO_PI)
+        per_position(turns[:, 0:1], 0, 1.0 / TWO_PI)
+        per_position(radians[:, 0:1], 2, 1.0)
+        highest_tables()
+        round_turns(nc.vector, 1)
+        round_turns(nc.gpsimd, 0)
+        reduce_turns(1)
+        low_tables(1)
         flipped = [flip_x(0, half) for half in range(2)]
-        group_x(nc.vector.tensor_copy, 0, 0, flipped[0])
-        quantise_x(0, 0)
-        group_x(nc.scalar.copy, 0, 1, flipped[1])
-        quantise_x(0, 1)
-        for f in (2, 1, 3):
-            sin_and_cos(f)
+        for half in range(2):
+            group_x(nc.vector.tensor_copy, 0, half, flipped[half])
+            quantise_x(0, half)
+        halves = (slice(0, SEQ // 2), slice(SEQ // 2, SEQ))
+        first_banks = [project(steps[0], cols) for cols in halves]
+        banks = {}
+        third_tables()
 
         def starts_sequence(s):
-            return s < len(steps) and steps[s][1:] == (0, 0)
+            return s < len(steps) and steps[s][1:] == (0, 1)
 
-        banks = {0: project(steps[0]), 1: project(steps[1])}
         for s in range(len(steps)):
             if starts_sequence(s + 4):
                 flipped = [flip_x(steps[s + 4][0], half) for half in range(2)]
             if starts_sequence(s + 3):
                 for half in range(2):
                     group_x(nc.scalar.copy, steps[s + 3][0], half, flipped[half])
-            b, w, f_low = steps[s]
-            f_high = f_low + HALF_TILES
-            low, high = banks[s]
-            done_low = rotate(nc.gpsimd, w, f_low, low, high)
-            last_adder = nc.vector if s == len(steps) - 1 else nc.gpsimd
-            done_high = rotate(last_adder, w, f_high, high, low)
+            b, w, j = steps[s]
+            product_low = parts.tile([P, 2, SEQ], F32, tag="product")
+            product_high = parts.tile([P, 2, SEQ], F32, tag="product")
+            products = (product_low, product_high)
+            summed = parts.tile([P, 2, GPSIMD_TILES * P], F32)
+            if s == 0:
+                for (low, high), cols in zip(first_banks, halves):
+                    multiply(w, j, 0, low, product_low, 0, 2, cols)
+                    multiply(w, j, 1, high, product_high, 0, 2, cols)
+                    if cols == halves[0]:
+                        banks[1] = project(steps[1])
+                add_parts(nc.gpsimd, products, summed, 0, 2)
+                reduce_turns(0)
+                low_tables(0)
+            elif s < len(steps) - 2:
+                low, high = banks[s]
+                multiply(w, j, 0, low, product_low, 0, 2)
+                multiply(w, j, 1, high, product_high, 0, 2)
+                add_parts(nc.gpsimd, products, summed, 0, 2)
+            else:
+                low, high = banks[s]
+                multiply(w, j, 0, low, product_low, 0, 1)
+                multiply(w, j, 1, high, product_high, 0, 1)
+                add_parts(nc.gpsimd, products, summed, 0, 1)
+                multiply(w, j, 1, high, product_high, 1, 1)
+                multiply(w, j, 0, low, product_low, 1, 1)
+                last_adder = nc.vector if s == len(steps) - 1 else nc.gpsimd
+                add_parts(last_adder, products, summed, 1, 1)
             if s + 2 < len(steps):
                 ahead = steps[s + 2]
                 if starts_sequence(s + 2):
                     quantise_x(ahead[0], 0)
                     quantise_x(ahead[0], 1)
                 banks[s + 2] = project(ahead)
-            turn_back_and_store(b, w, f_low, *done_low)
-            turn_back_and_store(b, w, f_high, *done_high)
+            turn_back_and_store(b, w, j, 0, products, summed)
+            turn_back_and_store(b, w, j, 1, products, summed)

@@ -25,7 +25,7 @@ F_TILES = FEAT // P
 T_TILES = SEQ // P
 HALF_TILES = F_TILES // 2
 TWO_PI = 2.0 * math.pi
-GPSIMD_TILES = 3
+GPSIMD_TILES = 2
 
 FLOPS = 2 * BATCH * SEQ * DIM * 2 * FEAT
 
@@ -233,25 +233,36 @@ def tile_ropemultiheadattention_pa_kernel(
                 in1=products[1][:, hs, 0 : GPSIMD_TILES * P], op=ALU.add,
             )
 
+        def turn_and_add(slot, products, h, t):
+            cols = slice(P * t, P * (t + 1))
+            nc.tensor.matmul(
+                out=slot, lhsT=products[0][:, h, cols], rhs=ident[:],
+                is_transpose=True, start=True, stop=False,
+            )
+            nc.tensor.matmul(
+                out=slot, lhsT=products[1][:, h, cols], rhs=ident[:],
+                is_transpose=True, start=False, stop=True,
+            )
+
+        def turn_sum(slot, summed, h, t):
+            nc.tensor.transpose(slot, summed[:, h, P * t : P * (t + 1)], ident[:])
+
+        def store(copy, b, w, f, back, first, count):
+            rows = parts.tile([P, T_TILES, P], F32)
+            copy(out=rows[:, 0:count, :], in_=back[:, 0:count, :])
+            out_rows = weights[w][3][b].rearrange("(n t) i -> n t i", t=T_TILES)
+            nc.sync.dma_start(
+                out=out_rows[:, first : first + count, P * f : P * (f + 1)],
+                in_=rows[:, 0:count, :],
+            )
+
         def turn_back_and_store(b, w, j, h, products, summed):
-            f = j + h * HALF_TILES
             back = psum_tr.tile([P, T_TILES, P], F32, tag="tr")
             for t in range(GPSIMD_TILES, T_TILES):
-                cols = slice(P * t, P * (t + 1))
-                nc.tensor.matmul(
-                    out=back[:, t, :], lhsT=products[0][:, h, cols], rhs=ident[:],
-                    is_transpose=True, start=True, stop=False,
-                )
-                nc.tensor.matmul(
-                    out=back[:, t, :], lhsT=products[1][:, h, cols], rhs=ident[:],
-                    is_transpose=True, start=False, stop=True,
-                )
+                turn_and_add(back[:, t, :], products, h, t)
             for t in range(GPSIMD_TILES):
-                nc.tensor.transpose(back[:, t, :], summed[:, h, P * t : P * (t + 1)], ident[:])
-            rows = parts.tile([P, T_TILES, P], F32)
-            nc.scalar.copy(out=rows[:], in_=back[:])
-            out_rows = weights[w][3][b].rearrange("(n t) i -> n t i", t=T_TILES)
-            nc.sync.dma_start(out=out_rows[:, :, P * f : P * (f + 1)], in_=rows[:])
+                turn_sum(back[:, t, :], summed, h, t)
+            store(nc.scalar.copy, b, w, j + h * HALF_TILES, back, 0, T_TILES)
 
         per_position(radians[:, 1:2], 3, 1.0)
         per_position(minus_radians[:, 1:2], 3, -1.0)
@@ -300,20 +311,41 @@ def tile_ropemultiheadattention_pa_kernel(
                 multiply(w, j, 0, low, product_low, 0, 2)
                 multiply(w, j, 1, high, product_high, 0, 2)
                 add_parts(nc.gpsimd, products, summed, 0, 2)
-            else:
+            elif s < len(steps) - 1:
                 low, high = banks[s]
                 multiply(w, j, 0, low, product_low, 0, 1)
                 multiply(w, j, 1, high, product_high, 0, 1)
                 add_parts(nc.gpsimd, products, summed, 0, 1)
                 multiply(w, j, 1, high, product_high, 1, 1)
                 multiply(w, j, 0, low, product_low, 1, 1)
-                last_adder = nc.vector if s == len(steps) - 1 else nc.gpsimd
-                add_parts(last_adder, products, summed, 1, 1)
+                add_parts(nc.gpsimd, products, summed, 1, 1)
+            else:
+                low, high = banks[s]
+                multiply(w, j, 0, low, product_low, 0, 1)
+                multiply(w, j, 1, high, product_high, 0, 1)
+                add_parts(nc.gpsimd, products, summed, 0, 1)
+                back_low = psum_tr.tile([P, T_TILES, P], F32, tag="tr")
+                for t in range(GPSIMD_TILES, T_TILES):
+                    turn_and_add(back_low[:, t, :], products, 0, t)
+                for half, cols in enumerate(halves):
+                    multiply(w, j, 1, high, product_high, 1, 1, cols)
+                    multiply(w, j, 0, low, product_low, 1, 1, cols)
+                    back_half = psum_tr.tile([P, T_TILES, P], F32, tag="tr")
+                    for t in range(2):
+                        turn_and_add(back_half[:, t, :], products, 1, 2 * half + t)
+                    if half == 0:
+                        store(nc.scalar.copy, b, w, j + HALF_TILES, back_half, 0, 2)
+                        for t in range(GPSIMD_TILES):
+                            turn_sum(back_low[:, t, :], summed, 0, t)
+                        store(nc.scalar.copy, b, w, j, back_low, 0, T_TILES)
+                    else:
+                        store(nc.vector.tensor_copy, b, w, j + HALF_TILES, back_half, 2, 2)
             if s + 2 < len(steps):
                 ahead = steps[s + 2]
                 if starts_sequence(s + 2):
                     quantise_x(ahead[0], 0)
                     quantise_x(ahead[0], 1)
                 banks[s + 2] = project(ahead)
-            turn_back_and_store(b, w, j, 0, products, summed)
-            turn_back_and_store(b, w, j, 1, products, summed)
+            if s < len(steps) - 1:
+                turn_back_and_store(b, w, j, 0, products, summed)
+                turn_back_and_store(b, w, j, 1, products, summed)

@@ -256,11 +256,11 @@ def tile_ropemultiheadattention_pa_kernel(
                 in_=rows[:, 0:count, :],
             )
 
-        def turn_back_and_store(b, w, j, h, products, summed):
+        def turn_back_and_store(b, w, j, h, products, summed, summed_tiles):
             back = psum_tr.tile([P, T_TILES, P], F32, tag="tr")
-            for t in range(GPSIMD_TILES, T_TILES):
+            for t in range(summed_tiles, T_TILES):
                 turn_and_add(back[:, t, :], products, h, t)
-            for t in range(GPSIMD_TILES):
+            for t in range(summed_tiles):
                 turn_sum(back[:, t, :], summed, h, t)
             store(nc.scalar.copy, b, w, j + h * HALF_TILES, back, 0, T_TILES)
 
@@ -293,24 +293,27 @@ def tile_ropemultiheadattention_pa_kernel(
                 for half in range(2):
                     group_x(nc.scalar.copy, steps[s + 3][0], half, flipped[half])
             b, w, j = steps[s]
+            port_wanted = s == 0 or starts_sequence(s + 2)
             product_low = parts.tile([P, 2, SEQ], F32, tag="product")
             product_high = parts.tile([P, 2, SEQ], F32, tag="product")
             products = (product_low, product_high)
-            summed = parts.tile([P, 2, GPSIMD_TILES * P], F32)
+            summed = None
+            if not port_wanted:
+                summed = parts.tile([P, 2, GPSIMD_TILES * P], F32)
             if s == 0:
                 for (low, high), cols in zip(first_banks, halves):
                     multiply(w, j, 0, low, product_low, 0, 2, cols)
                     multiply(w, j, 1, high, product_high, 0, 2, cols)
                     if cols == halves[0]:
                         banks[1] = project(steps[1])
-                add_parts(nc.gpsimd, products, summed, 0, 2)
                 reduce_turns(0)
                 low_tables(0)
             elif s < len(steps) - 2:
                 low, high = banks[s]
                 multiply(w, j, 0, low, product_low, 0, 2)
                 multiply(w, j, 1, high, product_high, 0, 2)
-                add_parts(nc.gpsimd, products, summed, 0, 2)
+                if not port_wanted:
+                    add_parts(nc.gpsimd, products, summed, 0, 2)
             elif s < len(steps) - 1:
                 low, high = banks[s]
                 multiply(w, j, 0, low, product_low, 0, 1)
@@ -347,5 +350,6 @@ def tile_ropemultiheadattention_pa_kernel(
                     quantise_x(ahead[0], 1)
                 banks[s + 2] = project(ahead)
             if s < len(steps) - 1:
-                turn_back_and_store(b, w, j, 0, products, summed)
-                turn_back_and_store(b, w, j, 1, products, summed)
+                summed_tiles = 0 if port_wanted else GPSIMD_TILES
+                turn_back_and_store(b, w, j, 0, products, summed, summed_tiles)
+                turn_back_and_store(b, w, j, 1, products, summed, summed_tiles)

@@ -25,7 +25,7 @@ F_TILES = FEAT // P
 T_TILES = SEQ // P
 HALF_TILES = F_TILES // 2
 TWO_PI = 2.0 * math.pi
-GPSIMD_TILES = 2
+GPSIMD_TILES = 1
 
 FLOPS = 2 * BATCH * SEQ * DIM * 2 * FEAT
 

@@ -26,6 +26,8 @@ T_TILES = SEQ // P
 HALF_TILES = F_TILES // 2
 TWO_PI = 2.0 * math.pi
 GPSIMD_TILES = 1
+ADD_STEPS = (0, 1, 2, 5, 6)
+GPSIMD_STEPS = (4,)
 
 FLOPS = 2 * BATCH * SEQ * DIM * 2 * FEAT
 
@@ -59,7 +61,7 @@ def tile_ropemultiheadattention_pa_kernel(
         table_warmer = keep.tile([P, 1], F32)
         turns = keep.tile([P, HALF_TILES], F32)
         radians = keep.tile([P, HALF_TILES], F32)
-        minus_radians = keep.tile([P, HALF_TILES], F32)
+        masked_row = keep.tile([P, F_TILES, P], F32)
         whole = keep.tile([P, HALF_TILES, SEQ], I32)
         frac = keep.tile([P, HALF_TILES, SEQ], F32)
         dist = keep.tile([P, F_TILES, SEQ], F32)
@@ -85,23 +87,6 @@ def tile_ropemultiheadattention_pa_kernel(
         nc.vector.memset(freq_row[:, 0:2], 1.0)
         nc.scalar.activation(out=table_warmer[:], in_=freq_row[:, 0:1], func=ACT.Sin)
         nc.vector.memset(w_planes[:].rearrange("p w n -> p (w n)").bitcast(I32), 0)
-        load_x(0)
-        with nc.allow_non_contiguous_dma(reason="1 KiB of bias, one element a partition"):
-            for w in range(2):
-                load_weight(w)
-                nc.sync.dma_start(
-                    out=bias[w][:], in_=weights[w][2].rearrange("(f p) -> p f", p=P)
-                )
-        load_x(1)
-
-        make_identity(nc, ident[:])
-        nc.gpsimd.iota(
-            pos[:],
-            pattern=[[1, T_TILES], [T_TILES, P]],
-            base=0,
-            channel_multiplier=0,
-            allow_small_or_imprecise_dtypes=True,
-        )
         for width in (2, 8, 32):
             for m in range(1, 4):
                 nc.vector.tensor_scalar_mul(
@@ -109,62 +94,90 @@ def tile_ropemultiheadattention_pa_kernel(
                     in0=freq_row[:, 0:width],
                     scalar1=ROPE_BASE ** (-(m * width) / FEAT),
                 )
-        freq_col = psum_tr.tile([P, T_TILES, P], F32, tag="tr")
-        nc.tensor.transpose(freq_col[:, 0, :], freq_row[:], ident[:])
+        for i in range(2):
+            load_x(i)
+            load_weight(i)
+            with nc.allow_non_contiguous_dma(reason="1 KiB of bias, one element a partition"):
+                nc.sync.dma_start(
+                    out=bias[i][:], in_=weights[i][2].rearrange("(f p) -> p f", p=P)
+                )
 
-        def per_position(out, f, factor):
-            nc.vector.tensor_scalar_mul(
-                out=out, in0=freq_col[:, 0, 0:1],
-                scalar1=factor * ROPE_BASE ** (-(f * P) / FEAT),
+        make_identity(nc, ident[:])
+        for half in range(2):
+            nc.gpsimd.iota(
+                pos[:, (SEQ // 2) * half : (SEQ // 2) * (half + 1)],
+                pattern=[[1, T_TILES // 2], [T_TILES, P]],
+                base=(T_TILES // 2) * half,
+                channel_multiplier=0,
+                allow_small_or_imprecise_dtypes=True,
             )
 
-        def round_turns(engine, j):
+        def per_position(out, f, factor):
+            nc.vector.scalar_tensor_tensor(
+                out=masked_row[:, f, :], in0=freq_row[:],
+                scalar=factor * ROPE_BASE ** (-(f * P) / FEAT), in1=ident[:],
+                op0=ALU.mult, op1=ALU.mult, accum_out=out,
+            )
+
+        def next_tile_down(out, per_position_above):
+            nc.vector.tensor_scalar_mul(
+                out=out, in0=per_position_above, scalar1=ROPE_BASE ** (P / FEAT)
+            )
+
+        everything = slice(0, SEQ)
+        halves = (slice(0, SEQ // 2), slice(SEQ // 2, SEQ))
+
+        def round_turns(engine, j, cols=everything):
             engine.tensor_scalar(
-                out=whole[:, j, :], in0=pos[:], scalar1=turns[:, j : j + 1], scalar2=0.0,
+                out=whole[:, j, cols], in0=pos[:, cols], scalar1=turns[:, j : j + 1], scalar2=0.0,
                 op0=ALU.mult, op1=ALU.add,
             )
 
-        def reduce_turns(j):
+        def reduce_turns(j, cols=everything):
             nc.vector.scalar_tensor_tensor(
-                out=frac[:, j, :], in0=pos[:], scalar=turns[:, j : j + 1], in1=whole[:, j, :],
-                op0=ALU.mult, op1=ALU.subtract,
+                out=frac[:, j, cols], in0=pos[:, cols], scalar=turns[:, j : j + 1],
+                in1=whole[:, j, cols], op0=ALU.mult, op1=ALU.subtract,
             )
 
-        def low_tables(j):
-            nc.scalar.activation(out=dist[:, j, :], in_=frac[:, j, :], func=ACT.Abs)
+        def low_tables(j, cols=everything):
+            nc.scalar.activation(out=dist[:, j, cols], in_=frac[:, j, cols], func=ACT.Abs)
             nc.scalar.activation(
-                out=from_low[:, j, 0, :], in_=dist[:, j, :], func=ACT.Sin, scale=-TWO_PI,
+                out=from_high[:, j, 0, cols], in_=frac[:, j, cols], func=ACT.Sin, scale=-TWO_PI
+            )
+            nc.scalar.activation(
+                out=from_low[:, j, 0, cols], in_=dist[:, j, cols], func=ACT.Sin, scale=-TWO_PI,
                 bias=math.pi / 2.0,
             )
+
+        def highest_tables(cols):
             nc.scalar.activation(
-                out=from_high[:, j, 0, :], in_=frac[:, j, :], func=ACT.Sin, scale=-TWO_PI
+                out=from_low[:, 1, 1, cols], in_=pos[:, cols], func=ACT.Sin,
+                scale=radians[:, 1:2],
+            )
+            nc.scalar.activation(
+                out=from_high[:, 1, 1, cols], in_=pos[:, cols], func=ACT.Sin,
+                scale=radians[:, 1:2],
+                bias=math.pi / 2.0,
             )
 
-        def highest_tables():
-            nc.scalar.activation(
-                out=from_low[:, 1, 1, :], in_=pos[:], func=ACT.Sin, scale=radians[:, 1:2]
-            )
-            nc.scalar.activation(
-                out=from_high[:, 1, 1, :], in_=pos[:], func=ACT.Sin,
-                scale=minus_radians[:, 1:2], bias=math.pi / 2.0,
-            )
-
-        def third_tables():
+        def third_tables(part):
+            if part == 1:
+                nc.scalar.activation(
+                    out=from_low[:, 0, 1, :], in_=dist[:, 2, :], func=ACT.Sin, scale=-1.0,
+                    bias=math.pi / 2.0,
+                )
+                nc.scalar.activation(
+                    out=from_high[:, 0, 1, :], in_=dist[:, 3, :], func=ACT.Sin, scale=1.0,
+                    bias=-math.pi / 2.0,
+                )
+                return
             nc.scalar.activation(
                 out=dist[:, 2, :], in_=pos[:], func=ACT.Abs, scale=radians[:, 0:1],
                 bias=-math.pi / 2.0,
             )
             nc.scalar.activation(
-                out=from_low[:, 0, 1, :], in_=dist[:, 2, :], func=ACT.Sin, scale=-1.0,
-                bias=math.pi / 2.0,
-            )
-            nc.scalar.activation(
                 out=dist[:, 3, :], in_=pos[:], func=ACT.Abs, scale=radians[:, 0:1],
                 bias=-math.pi,
-            )
-            nc.scalar.activation(
-                out=from_high[:, 0, 1, :], in_=dist[:, 3, :], func=ACT.Sin, scale=1.0,
-                bias=-math.pi / 2.0,
             )
 
         def flip_x(b, half):
@@ -198,7 +211,7 @@ def tile_ropemultiheadattention_pa_kernel(
                 in_=grouped[b][:, cols, :].rearrange("p c t -> p (c t)"),
             )
 
-        steps = [(b, w, j) for b in range(BATCH) for j in (1, 0) for w in range(2)]
+        steps = [(b, w, j) for j in (1, 0) for b in range(BATCH) for w in range(2)]
 
         def project(step, cols=slice(0, SEQ)):
             b, w, j = step
@@ -225,6 +238,20 @@ def tile_ropemultiheadattention_pa_kernel(
                 scalar=bias[w][:, f : f + 1],
                 in1=tables[side][:, j, first : first + count, cols], op0=ALU.add, op1=ALU.mult,
             )
+
+        def multiply_on_gpsimd(s):
+            b, w, j = steps[s]
+            f = j + HALF_TILES
+            biased = parts.tile([P, SEQ], F32, tag="biased")
+            nc.scalar.activation(
+                out=biased[:], in_=banks[s][1][:], func=ACT.Identity, bias=bias[w][:, f : f + 1]
+            )
+            product = parts.tile([P, 2, SEQ], F32, tag="gpsimd_product")
+            nc.gpsimd.tensor_tensor(
+                out=product[:], in0=biased[:].unsqueeze(1).to_broadcast([P, 2, SEQ]),
+                in1=tables[1][:, j, :, :], op=ALU.mult,
+            )
+            gpsimd_products[s] = product
 
         def add_parts(adder, products, summed, first, count):
             hs = slice(first, first + count)
@@ -264,71 +291,82 @@ def tile_ropemultiheadattention_pa_kernel(
                 turn_sum(back[:, t, :], summed, h, t)
             store(nc.scalar.copy, b, w, j + h * HALF_TILES, back, 0, T_TILES)
 
-        per_position(radians[:, 1:2], 3, 1.0)
-        per_position(minus_radians[:, 1:2], 3, -1.0)
         per_position(turns[:, 1:2], 1, 1.0 / TWO_PI)
-        per_position(turns[:, 0:1], 0, 1.0 / TWO_PI)
-        per_position(radians[:, 0:1], 2, 1.0)
-        highest_tables()
-        round_turns(nc.vector, 1)
-        round_turns(nc.gpsimd, 0)
-        reduce_turns(1)
-        low_tables(1)
+        per_position(radians[:, 1:2], 3, 1.0)
         flipped = [flip_x(0, half) for half in range(2)]
-        for half in range(2):
-            group_x(nc.vector.tensor_copy, 0, half, flipped[half])
-            quantise_x(0, half)
-        halves = (slice(0, SEQ // 2), slice(SEQ // 2, SEQ))
-        first_banks = [project(steps[0], cols) for cols in halves]
+        for cols in halves:
+            round_turns(nc.vector, 1, cols)
+        next_tile_down(turns[:, 0:1], turns[:, 1:2])
+        next_tile_down(radians[:, 0:1], radians[:, 1:2])
+        for cols in halves:
+            highest_tables(cols)
+            reduce_turns(1, cols)
+            low_tables(1, cols)
+            if cols == halves[0]:
+                group_x(nc.scalar.copy, 0, 1, flipped[1])
+        round_turns(nc.vector, 0)
+        group_x(nc.vector.tensor_copy, 0, 0, flipped[0])
+        quantise_x(0, 0)
+        reduce_turns(0)
+        quantise_x(0, 1)
+        first_banks = [project(steps[0], halves[0])]
+        flipped = [flip_x(1, 0)]
+        first_banks.append(project(steps[0], halves[1]))
         banks = {}
-        third_tables()
+        gpsimd_products = {}
 
-        def starts_sequence(s):
-            return s < len(steps) and steps[s][1:] == (0, 1)
-
+        last = len(steps) - 1
+        early_low = None
         for s in range(len(steps)):
-            if starts_sequence(s + 4):
-                flipped = [flip_x(steps[s + 4][0], half) for half in range(2)]
-            if starts_sequence(s + 3):
-                for half in range(2):
-                    group_x(nc.scalar.copy, steps[s + 3][0], half, flipped[half])
             b, w, j = steps[s]
-            port_wanted = s == 0 or starts_sequence(s + 2)
-            product_low = parts.tile([P, 2, SEQ], F32, tag="product")
-            product_high = parts.tile([P, 2, SEQ], F32, tag="product")
+            product_low = early_low if s == 1 else parts.tile([P, 2, SEQ], F32, tag="product")
+            if s in GPSIMD_STEPS:
+                product_high = gpsimd_products[s]
+            else:
+                product_high = parts.tile([P, 2, SEQ], F32, tag="product")
             products = (product_low, product_high)
             summed = None
-            if not port_wanted:
+            if s in ADD_STEPS:
                 summed = parts.tile([P, 2, GPSIMD_TILES * P], F32)
             if s == 0:
+                third_tables(0)
                 for (low, high), cols in zip(first_banks, halves):
                     multiply(w, j, 0, low, product_low, 0, 2, cols)
                     multiply(w, j, 1, high, product_high, 0, 2, cols)
                     if cols == halves[0]:
                         banks[1] = project(steps[1])
-                reduce_turns(0)
-                low_tables(0)
-            elif s < len(steps) - 2:
+                        flipped.append(flip_x(1, 1))
+                        for half in range(2):
+                            group_x(nc.scalar.copy, 1, half, flipped[half])
+                        third_tables(1)
+                early_low = parts.tile([P, 2, SEQ], F32, tag="product")
+                multiply(1, 1, 0, banks[1][0], early_low, 0, 2)
+                quantise_x(1, 0)
+                quantise_x(1, 1)
+            elif s < last - 1:
                 low, high = banks[s]
-                multiply(w, j, 0, low, product_low, 0, 2)
-                multiply(w, j, 1, high, product_high, 0, 2)
-                if not port_wanted:
-                    add_parts(nc.gpsimd, products, summed, 0, 2)
-            elif s < len(steps) - 1:
+                if s > 1:
+                    multiply(w, j, 0, low, product_low, 0, 2)
+                if s not in GPSIMD_STEPS:
+                    multiply(w, j, 1, high, product_high, 0, 2)
+            elif s < last:
                 low, high = banks[s]
                 multiply(w, j, 0, low, product_low, 0, 1)
-                multiply(w, j, 1, high, product_high, 0, 1)
-                add_parts(nc.gpsimd, products, summed, 0, 1)
-                multiply(w, j, 1, high, product_high, 1, 1)
+                if s not in GPSIMD_STEPS:
+                    multiply(w, j, 1, high, product_high, 0, 1)
+                if summed is not None:
+                    add_parts(nc.gpsimd, products, summed, 0, 1)
+                if s not in GPSIMD_STEPS:
+                    multiply(w, j, 1, high, product_high, 1, 1)
                 multiply(w, j, 0, low, product_low, 1, 1)
-                add_parts(nc.gpsimd, products, summed, 1, 1)
+                if summed is not None:
+                    add_parts(nc.gpsimd, products, summed, 1, 1)
             else:
                 low, high = banks[s]
                 multiply(w, j, 0, low, product_low, 0, 1)
                 multiply(w, j, 1, high, product_high, 0, 1)
-                add_parts(nc.gpsimd, products, summed, 0, 1)
                 back_low = psum_tr.tile([P, T_TILES, P], F32, tag="tr")
-                for t in range(GPSIMD_TILES, T_TILES):
+                for t in range(T_TILES):
                     turn_and_add(back_low[:, t, :], products, 0, t)
                 for half, cols in enumerate(halves):
                     multiply(w, j, 1, high, product_high, 1, 1, cols)
@@ -337,19 +375,21 @@ def tile_ropemultiheadattention_pa_kernel(
                     for t in range(2):
                         turn_and_add(back_half[:, t, :], products, 1, 2 * half + t)
                     if half == 0:
-                        store(nc.scalar.copy, b, w, j + HALF_TILES, back_half, 0, 2)
-                        for t in range(GPSIMD_TILES):
-                            turn_sum(back_low[:, t, :], summed, 0, t)
                         store(nc.scalar.copy, b, w, j, back_low, 0, T_TILES)
+                        store(nc.scalar.copy, b, w, j + HALF_TILES, back_half, 0, 2)
                     else:
                         store(nc.vector.tensor_copy, b, w, j + HALF_TILES, back_half, 2, 2)
-            if s + 2 < len(steps):
-                ahead = steps[s + 2]
-                if starts_sequence(s + 2):
-                    quantise_x(ahead[0], 0)
-                    quantise_x(ahead[0], 1)
-                banks[s + 2] = project(ahead)
-            if s < len(steps) - 1:
-                summed_tiles = 0 if port_wanted else GPSIMD_TILES
-                turn_back_and_store(b, w, j, 0, products, summed, summed_tiles)
-                turn_back_and_store(b, w, j, 1, products, summed, summed_tiles)
+                continue
+            if summed is not None and s < last - 1:
+                add_parts(nc.gpsimd, products, summed, 0, 2)
+            if 0 < s <= last - 2:
+                banks[s + 2] = project(steps[s + 2])
+            if s == 0:
+                low_tables(0)
+            if s == 2:
+                multiply_on_gpsimd(4)
+            summed_tiles = 0 if summed is None else GPSIMD_TILES
+            turn_back_and_store(b, w, j, 0, products, summed, summed_tiles)
+            turn_back_and_store(b, w, j, 1, products, summed, summed_tiles)
+            if s == 0:
+                banks[2] = project(steps[2])

@@ -20,14 +20,15 @@ SEQ = 512
 DIM = 512
 FEAT = 512
 ROPE_BASE = 10000.0
+ADD_STEPS = (0, 1, 2, 3, 6)
+GPSIMD_STEPS = (5,)
 PACK = 4
 F_TILES = FEAT // P
 T_TILES = SEQ // P
+HALF_T = T_TILES // 2
+HALF = SEQ // 2
 HALF_TILES = F_TILES // 2
 TWO_PI = 2.0 * math.pi
-GPSIMD_TILES = 1
-ADD_STEPS = (0, 1, 2, 5, 6)
-GPSIMD_STEPS = (4,)
 
 FLOPS = 2 * BATCH * SEQ * DIM * 2 * FEAT
 
@@ -69,11 +70,10 @@ def tile_ropemultiheadattention_pa_kernel(
         from_high = keep.tile([P, HALF_TILES, 2, SEQ], F32)
         tables = (from_low, from_high)
 
-        def load_x(b):
+        def load_x(b, half):
             x_rows = x[b].rearrange("(n t) k -> n t k", t=T_TILES)
-            for half in range(2):
-                ts = slice(2 * half, 2 * half + 2)
-                nc.sync.dma_start(out=x_sb[b][:, ts, :], in_=x_rows[:, ts, :])
+            ts = slice(HALF_T * half, HALF_T * (half + 1))
+            nc.sync.dma_start(out=x_sb[b][:, ts, :], in_=x_rows[:, ts, :])
 
         def load_weight(w):
             words, scales = weights[w][0], weights[w][1]
@@ -94,13 +94,15 @@ def tile_ropemultiheadattention_pa_kernel(
                     in0=freq_row[:, 0:width],
                     scalar1=ROPE_BASE ** (-(m * width) / FEAT),
                 )
-        for i in range(2):
-            load_x(i)
-            load_weight(i)
+        load_x(0, 0)
+        for w in range(2):
+            load_weight(w)
             with nc.allow_non_contiguous_dma(reason="1 KiB of bias, one element a partition"):
                 nc.sync.dma_start(
-                    out=bias[i][:], in_=weights[i][2].rearrange("(f p) -> p f", p=P)
+                    out=bias[w][:], in_=weights[w][2].rearrange("(f p) -> p f", p=P)
                 )
+        for b, half in ((1, 0), (0, 1), (1, 1)):
+            load_x(b, half)
 
         make_identity(nc, ident[:])
         for half in range(2):
@@ -124,60 +126,43 @@ def tile_ropemultiheadattention_pa_kernel(
                 out=out, in0=per_position_above, scalar1=ROPE_BASE ** (P / FEAT)
             )
 
-        everything = slice(0, SEQ)
-        halves = (slice(0, SEQ // 2), slice(SEQ // 2, SEQ))
+        halves = (slice(0, HALF), slice(HALF, SEQ))
 
-        def round_turns(engine, j, cols=everything):
-            engine.tensor_scalar(
+        def round_turns(j, cols):
+            nc.vector.tensor_scalar(
                 out=whole[:, j, cols], in0=pos[:, cols], scalar1=turns[:, j : j + 1], scalar2=0.0,
                 op0=ALU.mult, op1=ALU.add,
             )
 
-        def reduce_turns(j, cols=everything):
+        def reduce_turns(j, cols):
             nc.vector.scalar_tensor_tensor(
                 out=frac[:, j, cols], in0=pos[:, cols], scalar=turns[:, j : j + 1],
                 in1=whole[:, j, cols], op0=ALU.mult, op1=ALU.subtract,
             )
 
-        def low_tables(j, cols=everything):
-            nc.scalar.activation(out=dist[:, j, cols], in_=frac[:, j, cols], func=ACT.Abs)
-            nc.scalar.activation(
-                out=from_high[:, j, 0, cols], in_=frac[:, j, cols], func=ACT.Sin, scale=-TWO_PI
-            )
-            nc.scalar.activation(
-                out=from_low[:, j, 0, cols], in_=dist[:, j, cols], func=ACT.Sin, scale=-TWO_PI,
-                bias=math.pi / 2.0,
-            )
+        def sine(out, in_, scale, shift=0.0):
+            nc.scalar.activation(out=out, in_=in_, func=ACT.Sin, scale=scale, bias=shift)
 
-        def highest_tables(cols):
-            nc.scalar.activation(
-                out=from_low[:, 1, 1, cols], in_=pos[:, cols], func=ACT.Sin,
-                scale=radians[:, 1:2],
-            )
-            nc.scalar.activation(
-                out=from_high[:, 1, 1, cols], in_=pos[:, cols], func=ACT.Sin,
-                scale=radians[:, 1:2],
-                bias=math.pi / 2.0,
-            )
+        def tables_of_pair_1(cols):
+            sine(from_low[:, 1, 1, cols], pos[:, cols], radians[:, 1:2])
+            nc.scalar.activation(out=dist[:, 1, cols], in_=frac[:, 1, cols], func=ACT.Abs)
+            sine(from_high[:, 1, 1, cols], pos[:, cols], radians[:, 1:2], math.pi / 2.0)
+            sine(from_low[:, 1, 0, cols], dist[:, 1, cols], -TWO_PI, math.pi / 2.0)
+            sine(from_high[:, 1, 0, cols], frac[:, 1, cols], -TWO_PI)
 
-        def third_tables(part):
-            if part == 1:
-                nc.scalar.activation(
-                    out=from_low[:, 0, 1, :], in_=dist[:, 2, :], func=ACT.Sin, scale=-1.0,
-                    bias=math.pi / 2.0,
-                )
-                nc.scalar.activation(
-                    out=from_high[:, 0, 1, :], in_=dist[:, 3, :], func=ACT.Sin, scale=1.0,
-                    bias=-math.pi / 2.0,
-                )
-                return
+        def tables_of_pair_0(cols):
+            nc.scalar.activation(out=dist[:, 0, cols], in_=frac[:, 0, cols], func=ACT.Abs)
+            distance(2, cols, -math.pi / 2.0)
+            sine(from_low[:, 0, 0, cols], dist[:, 0, cols], -TWO_PI, math.pi / 2.0)
+            sine(from_low[:, 0, 1, cols], dist[:, 2, cols], -1.0, math.pi / 2.0)
+            distance(3, cols, -math.pi)
+            sine(from_high[:, 0, 0, cols], frac[:, 0, cols], -TWO_PI)
+            sine(from_high[:, 0, 1, cols], dist[:, 3, cols], 1.0, -math.pi / 2.0)
+
+        def distance(i, cols, shift):
             nc.scalar.activation(
-                out=dist[:, 2, :], in_=pos[:], func=ACT.Abs, scale=radians[:, 0:1],
-                bias=-math.pi / 2.0,
-            )
-            nc.scalar.activation(
-                out=dist[:, 3, :], in_=pos[:], func=ACT.Abs, scale=radians[:, 0:1],
-                bias=-math.pi,
+                out=dist[:, i, cols], in_=pos[:, cols], func=ACT.Abs, scale=radians[:, 0:1],
+                bias=shift,
             )
 
         def flip_x(b, half):
@@ -211,185 +196,153 @@ def tile_ropemultiheadattention_pa_kernel(
                 in_=grouped[b][:, cols, :].rearrange("p c t -> p (c t)"),
             )
 
-        steps = [(b, w, j) for j in (1, 0) for b in range(BATCH) for w in range(2)]
+        steps = [(half, b, w) for half in range(2) for b in range(BATCH) for w in range(2)]
+        last = len(steps) - 1
 
-        def project(step, cols=slice(0, SEQ)):
-            b, w, j = step
-            banks = []
-            for f in (j, j + HALF_TILES):
-                acc = psum_mx.tile([P, SEQ], F32, tag="acc")
-                nc.tensor.matmul_mx(
-                    out=acc[:, cols],
-                    lhsT=w_words[:, w, 2 * P * f : 2 * P * (f + 1)].bitcast(FP4X4),
-                    lhsT_scale=w_planes[:, w, P * f : P * (f + 1)],
-                    rhs=x_codes[:, b, cols].bitcast(FP8X4),
-                    rhs_scale=x_planes[:, b, cols],
-                    start=True,
-                    stop=True,
-                )
-                banks.append(acc)
+        def project(s):
+            half, b, w = steps[s]
+            cols = halves[half]
+            banks = [None, None]
+            for j in (1, 0):
+                acc = psum_mx.tile([P, 2, HALF], F32, tag="acc")
+                for side in range(2):
+                    f = j + side * HALF_TILES
+                    nc.tensor.matmul_mx(
+                        out=acc[:, side, :],
+                        lhsT=w_words[:, w, 2 * P * f : 2 * P * (f + 1)].bitcast(FP4X4),
+                        lhsT_scale=w_planes[:, w, P * f : P * (f + 1)],
+                        rhs=x_codes[:, b, cols].bitcast(FP8X4),
+                        rhs_scale=x_planes[:, b, cols],
+                        start=True,
+                        stop=True,
+                    )
+                banks[j] = acc
             return banks
 
-        def multiply(w, j, side, acc, product, first, count, cols=slice(0, SEQ)):
+        def multiply(s, j, side, acc, product, first=0, last_col=HALF):
+            half, b, w = steps[s]
             f = j + side * HALF_TILES
+            cols = slice(first, last_col)
+            in_table = slice(HALF * half + first, HALF * half + last_col)
             nc.vector.scalar_tensor_tensor(
-                out=product[:, first : first + count, cols],
-                in0=acc[:, cols].unsqueeze(1).to_broadcast([P, count, cols.stop - cols.start]),
+                out=product[:, :, cols],
+                in0=acc[:, side, cols].unsqueeze(1).to_broadcast([P, 2, last_col - first]),
                 scalar=bias[w][:, f : f + 1],
-                in1=tables[side][:, j, first : first + count, cols], op0=ALU.add, op1=ALU.mult,
+                in1=tables[side][:, j, :, in_table], op0=ALU.add, op1=ALU.mult,
             )
 
+        def new_product():
+            return parts.tile([P, 2, HALF], F32, name="product", tag="product", bufs=16)
+
         def multiply_on_gpsimd(s):
-            b, w, j = steps[s]
-            f = j + HALF_TILES
-            biased = parts.tile([P, SEQ], F32, tag="biased")
+            half, b, w = steps[s]
+            biased = parts.tile([P, HALF], F32, tag="biased")
             nc.scalar.activation(
-                out=biased[:], in_=banks[s][1][:], func=ACT.Identity, bias=bias[w][:, f : f + 1]
+                out=biased[:], in_=banks[s][0][:, 1, :], func=ACT.Identity,
+                bias=bias[w][:, HALF_TILES : HALF_TILES + 1],
             )
-            product = parts.tile([P, 2, SEQ], F32, tag="gpsimd_product")
+            product = parts.tile([P, 2, HALF], F32, tag="gpsimd_product")
             nc.gpsimd.tensor_tensor(
-                out=product[:], in0=biased[:].unsqueeze(1).to_broadcast([P, 2, SEQ]),
-                in1=tables[1][:, j, :, :], op=ALU.mult,
+                out=product[:], in0=biased[:].unsqueeze(1).to_broadcast([P, 2, HALF]),
+                in1=from_high[:, 0, :, halves[half]], op=ALU.mult,
             )
             gpsimd_products[s] = product
 
-        def add_parts(adder, products, summed, first, count):
-            hs = slice(first, first + count)
-            adder.tensor_tensor(
-                out=summed[:, hs, :], in0=products[0][:, hs, 0 : GPSIMD_TILES * P],
-                in1=products[1][:, hs, 0 : GPSIMD_TILES * P], op=ALU.add,
-            )
-
-        def turn_and_add(slot, products, h, t):
+        def turn_and_add(slot, pair, h, t):
             cols = slice(P * t, P * (t + 1))
             nc.tensor.matmul(
-                out=slot, lhsT=products[0][:, h, cols], rhs=ident[:],
+                out=slot, lhsT=pair[0][:, h, cols], rhs=ident[:],
                 is_transpose=True, start=True, stop=False,
             )
             nc.tensor.matmul(
-                out=slot, lhsT=products[1][:, h, cols], rhs=ident[:],
+                out=slot, lhsT=pair[1][:, h, cols], rhs=ident[:],
                 is_transpose=True, start=False, stop=True,
             )
 
-        def turn_sum(slot, summed, h, t):
-            nc.tensor.transpose(slot, summed[:, h, P * t : P * (t + 1)], ident[:])
+        def turn_tile(s, t, products, summed):
+            back = psum_tr.tile([P, FEAT], F32, tag="tr")
+            for j in (1, 0):
+                for h in range(2):
+                    f = j + h * HALF_TILES
+                    slot = back[:, P * f : P * (f + 1)]
+                    if summed is not None and j == 1 and t == 0:
+                        nc.tensor.transpose(slot, summed[:, h, :], ident[:])
+                    else:
+                        turn_and_add(slot, products[j], h, t)
+            return back
 
-        def store(copy, b, w, f, back, first, count):
-            rows = parts.tile([P, T_TILES, P], F32)
-            copy(out=rows[:, 0:count, :], in_=back[:, 0:count, :])
+        def store(s, t, back, copy):
+            half, b, w = steps[s]
+            rows = parts.tile([P, FEAT], F32, tag="rows", bufs=12)
+            copy(out=rows[:], in_=back[:])
             out_rows = weights[w][3][b].rearrange("(n t) i -> n t i", t=T_TILES)
-            nc.sync.dma_start(
-                out=out_rows[:, first : first + count, P * f : P * (f + 1)],
-                in_=rows[:, 0:count, :],
-            )
-
-        def turn_back_and_store(b, w, j, h, products, summed, summed_tiles):
-            back = psum_tr.tile([P, T_TILES, P], F32, tag="tr")
-            for t in range(summed_tiles, T_TILES):
-                turn_and_add(back[:, t, :], products, h, t)
-            for t in range(summed_tiles):
-                turn_sum(back[:, t, :], summed, h, t)
-            store(nc.scalar.copy, b, w, j + h * HALF_TILES, back, 0, T_TILES)
+            nc.sync.dma_start(out=out_rows[:, HALF_T * half + t, :], in_=rows[:])
 
         per_position(turns[:, 1:2], 1, 1.0 / TWO_PI)
         per_position(radians[:, 1:2], 3, 1.0)
-        flipped = [flip_x(0, half) for half in range(2)]
-        for cols in halves:
-            round_turns(nc.vector, 1, cols)
+        round_turns(1, halves[0])
         next_tile_down(turns[:, 0:1], turns[:, 1:2])
         next_tile_down(radians[:, 0:1], radians[:, 1:2])
-        for cols in halves:
-            highest_tables(cols)
-            reduce_turns(1, cols)
-            low_tables(1, cols)
-            if cols == halves[0]:
-                group_x(nc.scalar.copy, 0, 1, flipped[1])
-        round_turns(nc.vector, 0)
-        group_x(nc.vector.tensor_copy, 0, 0, flipped[0])
+        round_turns(0, halves[0])
+        reduce_turns(1, halves[0])
+        reduce_turns(0, halves[0])
+        tables_of_pair_1(halves[0])
+        tables_of_pair_0(halves[0])
+        flipped = flip_x(0, 0)
+        group_x(nc.vector.tensor_copy, 0, 0, flipped)
+        for j in (1, 0):
+            round_turns(j, halves[1])
         quantise_x(0, 0)
-        reduce_turns(0)
-        quantise_x(0, 1)
-        first_banks = [project(steps[0], halves[0])]
-        flipped = [flip_x(1, 0)]
-        first_banks.append(project(steps[0], halves[1]))
-        banks = {}
-        gpsimd_products = {}
+        banks = {0: project(0)}
+        for j in (1, 0):
+            reduce_turns(j, halves[1])
+        flipped = flip_x(1, 0)
+        group_x(nc.scalar.copy, 1, 0, flipped)
+        tables_of_pair_1(halves[1])
+        banks[1] = project(1)
 
-        last = len(steps) - 1
-        early_low = None
+        gpsimd_products = {}
         for s in range(len(steps)):
-            b, w, j = steps[s]
-            product_low = early_low if s == 1 else parts.tile([P, 2, SEQ], F32, tag="product")
+            products = [[new_product(), new_product()] for j in range(HALF_TILES)]
             if s in GPSIMD_STEPS:
-                product_high = gpsimd_products[s]
-            else:
-                product_high = parts.tile([P, 2, SEQ], F32, tag="product")
-            products = (product_low, product_high)
+                products[0][1] = gpsimd_products[s]
             summed = None
             if s in ADD_STEPS:
-                summed = parts.tile([P, 2, GPSIMD_TILES * P], F32)
-            if s == 0:
-                third_tables(0)
-                for (low, high), cols in zip(first_banks, halves):
-                    multiply(w, j, 0, low, product_low, 0, 2, cols)
-                    multiply(w, j, 1, high, product_high, 0, 2, cols)
-                    if cols == halves[0]:
-                        banks[1] = project(steps[1])
-                        flipped.append(flip_x(1, 1))
-                        for half in range(2):
-                            group_x(nc.scalar.copy, 1, half, flipped[half])
-                        third_tables(1)
-                early_low = parts.tile([P, 2, SEQ], F32, tag="product")
-                multiply(1, 1, 0, banks[1][0], early_low, 0, 2)
-                quantise_x(1, 0)
-                quantise_x(1, 1)
-            elif s < last - 1:
-                low, high = banks[s]
-                if s > 1:
-                    multiply(w, j, 0, low, product_low, 0, 2)
-                if s not in GPSIMD_STEPS:
-                    multiply(w, j, 1, high, product_high, 0, 2)
-            elif s < last:
-                low, high = banks[s]
-                multiply(w, j, 0, low, product_low, 0, 1)
-                if s not in GPSIMD_STEPS:
-                    multiply(w, j, 1, high, product_high, 0, 1)
-                if summed is not None:
-                    add_parts(nc.gpsimd, products, summed, 0, 1)
-                if s not in GPSIMD_STEPS:
-                    multiply(w, j, 1, high, product_high, 1, 1)
-                multiply(w, j, 0, low, product_low, 1, 1)
-                if summed is not None:
-                    add_parts(nc.gpsimd, products, summed, 1, 1)
+                summed = parts.tile([P, 2, P], F32)
+            if s < last:
+                for j in (1, 0):
+                    for side in range(2):
+                        if not (s in GPSIMD_STEPS and (j, side) == (0, 1)):
+                            multiply(s, j, side, banks[s][j], products[j][side])
+                    if j == 1 and summed is not None:
+                        nc.gpsimd.tensor_tensor(
+                            out=summed[:], in0=products[1][0][:, :, 0:P],
+                            in1=products[1][1][:, :, 0:P], op=ALU.add,
+                        )
             else:
-                low, high = banks[s]
-                multiply(w, j, 0, low, product_low, 0, 1)
-                multiply(w, j, 1, high, product_high, 0, 1)
-                back_low = psum_tr.tile([P, T_TILES, P], F32, tag="tr")
-                for t in range(T_TILES):
-                    turn_and_add(back_low[:, t, :], products, 0, t)
-                for half, cols in enumerate(halves):
-                    multiply(w, j, 1, high, product_high, 1, 1, cols)
-                    multiply(w, j, 0, low, product_low, 1, 1, cols)
-                    back_half = psum_tr.tile([P, T_TILES, P], F32, tag="tr")
-                    for t in range(2):
-                        turn_and_add(back_half[:, t, :], products, 1, 2 * half + t)
-                    if half == 0:
-                        store(nc.scalar.copy, b, w, j, back_low, 0, T_TILES)
-                        store(nc.scalar.copy, b, w, j + HALF_TILES, back_half, 0, 2)
-                    else:
-                        store(nc.vector.tensor_copy, b, w, j + HALF_TILES, back_half, 2, 2)
-                continue
-            if summed is not None and s < last - 1:
-                add_parts(nc.gpsimd, products, summed, 0, 2)
-            if 0 < s <= last - 2:
-                banks[s + 2] = project(steps[s + 2])
+                for t in range(HALF_T):
+                    for j in (1, 0):
+                        for side in range(2):
+                            multiply(
+                                s, j, side, banks[s][j], products[j][side], P * t, P * (t + 1)
+                            )
+            if s + 2 <= last:
+                half, b, w = steps[s + 2]
+                if w == 0:
+                    quantise_x(b, half)
+                if s > 0:
+                    banks[s + 2] = project(s + 2)
+                    if s + 2 in GPSIMD_STEPS:
+                        multiply_on_gpsimd(s + 2)
+            if s in (0, 2):
+                half, b, w = steps[s + 4]
+                flipped = flip_x(b, half)
+            for t in range(HALF_T):
+                back = turn_tile(s, t, products, summed)
+                store(s, t, back, nc.scalar.copy if s < last or t == 0 else nc.vector.tensor_copy)
             if s == 0:
-                low_tables(0)
-            if s == 2:
-                multiply_on_gpsimd(4)
-            summed_tiles = 0 if summed is None else GPSIMD_TILES
-            turn_back_and_store(b, w, j, 0, products, summed, summed_tiles)
-            turn_back_and_store(b, w, j, 1, products, summed, summed_tiles)
+                banks[2] = project(2)
+            if s in (0, 2):
+                group_x(nc.scalar.copy, b, half, flipped)
             if s == 0:
-                banks[2] = project(steps[2])
+                tables_of_pair_0(halves[1])

@@ -20,8 +20,9 @@ SEQ = 512
 DIM = 512
 FEAT = 512
 ROPE_BASE = 10000.0
-ADD_STEPS = (0, 1, 2, 3, 6)
-GPSIMD_STEPS = (5,)
+ADD_STEPS = (0, 1, 4, 5, 6, 7)
+GPSIMD_STEPS = (3,)
+GPSIMD_T = (1, 1, 1, 1, 1, 2, 2, 1)
 PACK = 4
 F_TILES = FEAT // P
 T_TILES = SEQ // P
@@ -143,21 +144,41 @@ def tile_ropemultiheadattention_pa_kernel(
         def sine(out, in_, scale, shift=0.0):
             nc.scalar.activation(out=out, in_=in_, func=ACT.Sin, scale=scale, bias=shift)
 
-        def tables_of_pair_1(cols):
+        def absolute(tiles, cols):
+            nc.scalar.activation(
+                out=dist[:, tiles, cols], in_=frac[:, tiles, cols], func=ACT.Abs
+            )
+
+        def first_tables():
+            cols = halves[0]
             sine(from_low[:, 1, 1, cols], pos[:, cols], radians[:, 1:2])
-            nc.scalar.activation(out=dist[:, 1, cols], in_=frac[:, 1, cols], func=ACT.Abs)
             sine(from_high[:, 1, 1, cols], pos[:, cols], radians[:, 1:2], math.pi / 2.0)
+            distance(2, cols, -math.pi / 2.0)
+            absolute(1, cols)
             sine(from_low[:, 1, 0, cols], dist[:, 1, cols], -TWO_PI, math.pi / 2.0)
             sine(from_high[:, 1, 0, cols], frac[:, 1, cols], -TWO_PI)
-
-        def tables_of_pair_0(cols):
-            nc.scalar.activation(out=dist[:, 0, cols], in_=frac[:, 0, cols], func=ACT.Abs)
-            distance(2, cols, -math.pi / 2.0)
-            sine(from_low[:, 0, 0, cols], dist[:, 0, cols], -TWO_PI, math.pi / 2.0)
+            absolute(0, cols)
             sine(from_low[:, 0, 1, cols], dist[:, 2, cols], -1.0, math.pi / 2.0)
+            sine(from_low[:, 0, 0, cols], dist[:, 0, cols], -TWO_PI, math.pi / 2.0)
             distance(3, cols, -math.pi)
             sine(from_high[:, 0, 0, cols], frac[:, 0, cols], -TWO_PI)
             sine(from_high[:, 0, 1, cols], dist[:, 3, cols], 1.0, -math.pi / 2.0)
+
+        def later_tables(lot):
+            cols = halves[1]
+            low_tiles = slice(0, HALF_TILES)
+            if lot == 0:
+                sine(from_low[:, 1, 1, cols], pos[:, cols], radians[:, 1:2])
+                sine(from_high[:, 1, 1, cols], pos[:, cols], radians[:, 1:2], math.pi / 2.0)
+                sine(from_high[:, :, 0, cols], frac[:, low_tiles, cols], -TWO_PI)
+            elif lot == 1:
+                absolute(low_tiles, cols)
+                distance(2, cols, -math.pi / 2.0)
+                sine(from_low[:, :, 0, cols], dist[:, low_tiles, cols], -TWO_PI, math.pi / 2.0)
+                distance(3, cols, -math.pi)
+            else:
+                sine(from_low[:, 0, 1, cols], dist[:, 2, cols], -1.0, math.pi / 2.0)
+                sine(from_high[:, 0, 1, cols], dist[:, 3, cols], 1.0, -math.pi / 2.0)
 
         def distance(i, cols, shift):
             nc.scalar.activation(
@@ -165,10 +186,12 @@ def tile_ropemultiheadattention_pa_kernel(
                 bias=shift,
             )
 
-        def flip_x(b, half):
+        both_tiles = range(HALF_T)
+
+        def flip_x(b, half, tiles=both_tiles):
             x_words = x_sb[b][:].rearrange("p t k -> p (t k)").bitcast(F32)
             flipped = psum_tr.tile([P, T_TILES, P], F32, tag="tr")
-            for tl in range(2):
+            for tl in tiles:
                 first = (DIM // 2) * (2 * half + tl)
                 for u in range(2):
                     nc.tensor.transpose(
@@ -178,14 +201,15 @@ def tile_ropemultiheadattention_pa_kernel(
                     )
             return flipped
 
-        def group_x(copy, b, half, flipped):
+        def group_x(copy, b, half, flipped, tiles=both_tiles):
+            tiles = slice(tiles.start, tiles.stop)
             grouped_words = (
                 grouped[b][:].rearrange("p c t -> p (c t)").bitcast(F32)
                 .rearrange("p (h t n u) -> p h t n u", h=2, t=2, u=2)
             )
             copy(
-                out=grouped_words[:, half],
-                in_=flipped[:].rearrange("p (t u) n -> p t n u", u=2),
+                out=grouped_words[:, half, tiles],
+                in_=flipped[:].rearrange("p (t u) n -> p t n u", u=2)[:, tiles],
             )
 
         def quantise_x(b, half):
@@ -199,16 +223,20 @@ def tile_ropemultiheadattention_pa_kernel(
         steps = [(half, b, w) for half in range(2) for b in range(BATCH) for w in range(2)]
         last = len(steps) - 1
 
-        def project(s):
+        def project(s, bank_a_tile=False):
             half, b, w = steps[s]
             cols = halves[half]
             banks = [None, None]
             for j in (1, 0):
                 acc = psum_mx.tile([P, 2, HALF], F32, tag="acc")
+                sides = [acc[:, 0, :], acc[:, 1, :]]
+                if bank_a_tile:
+                    other = psum_mx.tile([P, 2, HALF], F32, tag="acc")
+                    sides[1] = other[:, 1, :]
                 for side in range(2):
                     f = j + side * HALF_TILES
                     nc.tensor.matmul_mx(
-                        out=acc[:, side, :],
+                        out=sides[side],
                         lhsT=w_words[:, w, 2 * P * f : 2 * P * (f + 1)].bitcast(FP4X4),
                         lhsT_scale=w_planes[:, w, P * f : P * (f + 1)],
                         rhs=x_codes[:, b, cols].bitcast(FP8X4),
@@ -216,7 +244,7 @@ def tile_ropemultiheadattention_pa_kernel(
                         start=True,
                         stop=True,
                     )
-                banks[j] = acc
+                banks[j] = sides
             return banks
 
         def multiply(s, j, side, acc, product, first=0, last_col=HALF):
@@ -226,7 +254,7 @@ def tile_ropemultiheadattention_pa_kernel(
             in_table = slice(HALF * half + first, HALF * half + last_col)
             nc.vector.scalar_tensor_tensor(
                 out=product[:, :, cols],
-                in0=acc[:, side, cols].unsqueeze(1).to_broadcast([P, 2, last_col - first]),
+                in0=acc[side][:, cols].unsqueeze(1).to_broadcast([P, 2, last_col - first]),
                 scalar=bias[w][:, f : f + 1],
                 in1=tables[side][:, j, :, in_table], op0=ALU.add, op1=ALU.mult,
             )
@@ -238,7 +266,7 @@ def tile_ropemultiheadattention_pa_kernel(
             half, b, w = steps[s]
             biased = parts.tile([P, HALF], F32, tag="biased")
             nc.scalar.activation(
-                out=biased[:], in_=banks[s][0][:, 1, :], func=ACT.Identity,
+                out=biased[:], in_=banks[s][0][1], func=ACT.Identity,
                 bias=bias[w][:, HALF_TILES : HALF_TILES + 1],
             )
             product = parts.tile([P, 2, HALF], F32, tag="gpsimd_product")
@@ -247,6 +275,12 @@ def tile_ropemultiheadattention_pa_kernel(
                 in1=from_high[:, 0, :, halves[half]], op=ALU.mult,
             )
             gpsimd_products[s] = product
+
+        def add_on_gpsimd(summed, pair, tiles):
+            nc.gpsimd.tensor_tensor(
+                out=summed[:], in0=pair[0][:, :, 0 : P * tiles], in1=pair[1][:, :, 0 : P * tiles],
+                op=ALU.add,
+            )
 
         def turn_and_add(slot, pair, h, t):
             cols = slice(P * t, P * (t + 1))
@@ -259,24 +293,26 @@ def tile_ropemultiheadattention_pa_kernel(
                 is_transpose=True, start=False, stop=True,
             )
 
-        def turn_tile(s, t, products, summed):
+        def turn_tile(s, t, products, summed, hs=(0, 1)):
             back = psum_tr.tile([P, FEAT], F32, tag="tr")
             for j in (1, 0):
-                for h in range(2):
+                for h in hs:
                     f = j + h * HALF_TILES
                     slot = back[:, P * f : P * (f + 1)]
-                    if summed is not None and j == 1 and t == 0:
-                        nc.tensor.transpose(slot, summed[:, h, :], ident[:])
+                    if summed is not None and j == 1 and t < summed.shape[2] // P:
+                        nc.tensor.transpose(slot, summed[:, h, P * t : P * (t + 1)], ident[:])
                     else:
                         turn_and_add(slot, products[j], h, t)
             return back
 
-        def store(s, t, back, copy):
+        def store(s, t, back, copy, features=slice(0, FEAT)):
             half, b, w = steps[s]
             rows = parts.tile([P, FEAT], F32, tag="rows", bufs=12)
-            copy(out=rows[:], in_=back[:])
+            copy(out=rows[:, features], in_=back[:, features])
             out_rows = weights[w][3][b].rearrange("(n t) i -> n t i", t=T_TILES)
-            nc.sync.dma_start(out=out_rows[:, HALF_T * half + t, :], in_=rows[:])
+            nc.sync.dma_start(
+                out=out_rows[:, HALF_T * half + t, features], in_=rows[:, features]
+            )
 
         per_position(turns[:, 1:2], 1, 1.0 / TWO_PI)
         per_position(radians[:, 1:2], 3, 1.0)
@@ -285,40 +321,43 @@ def tile_ropemultiheadattention_pa_kernel(
         next_tile_down(radians[:, 0:1], radians[:, 1:2])
         round_turns(0, halves[0])
         reduce_turns(1, halves[0])
+        for t in both_tiles:
+            one_tile = range(t, t + 1)
+            flipped = flip_x(0, 0, one_tile)
+            group_x(nc.vector.tensor_copy, 0, 0, flipped, one_tile)
         reduce_turns(0, halves[0])
-        tables_of_pair_1(halves[0])
-        tables_of_pair_0(halves[0])
-        flipped = flip_x(0, 0)
-        group_x(nc.vector.tensor_copy, 0, 0, flipped)
+        first_tables()
+        quantise_x(0, 0)
+        banks = {0: project(0, True)}
         for j in (1, 0):
             round_turns(j, halves[1])
-        quantise_x(0, 0)
-        banks = {0: project(0)}
         for j in (1, 0):
             reduce_turns(j, halves[1])
         flipped = flip_x(1, 0)
         group_x(nc.scalar.copy, 1, 0, flipped)
-        tables_of_pair_1(halves[1])
+        later_tables(0)
         banks[1] = project(1)
 
         gpsimd_products = {}
+        if 1 in GPSIMD_STEPS:
+            multiply_on_gpsimd(1)
         for s in range(len(steps)):
             products = [[new_product(), new_product()] for j in range(HALF_TILES)]
             if s in GPSIMD_STEPS:
                 products[0][1] = gpsimd_products[s]
             summed = None
             if s in ADD_STEPS:
-                summed = parts.tile([P, 2, P], F32)
+                tiles = GPSIMD_T[s]
+                summed = parts.tile([P, 2, tiles * P], F32, name="summed", tag="summed%d" % tiles)
             if s < last:
                 for j in (1, 0):
+                    if j == 0 and s == 2:
+                        quantise_x(steps[s + 2][1], steps[s + 2][0])
                     for side in range(2):
                         if not (s in GPSIMD_STEPS and (j, side) == (0, 1)):
                             multiply(s, j, side, banks[s][j], products[j][side])
                     if j == 1 and summed is not None:
-                        nc.gpsimd.tensor_tensor(
-                            out=summed[:], in0=products[1][0][:, :, 0:P],
-                            in1=products[1][1][:, :, 0:P], op=ALU.add,
-                        )
+                        add_on_gpsimd(summed, products[1], tiles)
             else:
                 for t in range(HALF_T):
                     for j in (1, 0):
@@ -326,23 +365,31 @@ def tile_ropemultiheadattention_pa_kernel(
                             multiply(
                                 s, j, side, banks[s][j], products[j][side], P * t, P * (t + 1)
                             )
+                        if summed is not None and j == 1 and t == 0:
+                            add_on_gpsimd(summed, products[1], 1)
             if s + 2 <= last:
                 half, b, w = steps[s + 2]
-                if w == 0:
+                if w == 0 and s != 2:
                     quantise_x(b, half)
                 if s > 0:
                     banks[s + 2] = project(s + 2)
                     if s + 2 in GPSIMD_STEPS:
                         multiply_on_gpsimd(s + 2)
-            if s in (0, 2):
-                half, b, w = steps[s + 4]
+            if s < 2:
+                half, b, w = steps[2 * s + 4]
                 flipped = flip_x(b, half)
             for t in range(HALF_T):
-                back = turn_tile(s, t, products, summed)
-                store(s, t, back, nc.scalar.copy if s < last or t == 0 else nc.vector.tensor_copy)
+                if s < last or t < HALF_T - 1:
+                    store(s, t, turn_tile(s, t, products, summed), nc.scalar.copy)
+                else:
+                    for h, copy in enumerate((nc.scalar.copy, nc.vector.tensor_copy)):
+                        features = slice(FEAT // 2 * h, FEAT // 2 * (h + 1))
+                        store(s, t, turn_tile(s, t, products, summed, (h,)), copy, features)
             if s == 0:
                 banks[2] = project(2)
-            if s in (0, 2):
+                if 2 in GPSIMD_STEPS:
+                    multiply_on_gpsimd(2)
+            if s < 2:
                 group_x(nc.scalar.copy, b, half, flipped)
-            if s == 0:
-                tables_of_pair_0(halves[1])
+            if s < 2:
+                later_tables(s + 1)

import math
from contextlib import ExitStack

import concourse.mybir as mybir
from concourse.masks import make_identity

F32 = mybir.dt.float32
BF16 = mybir.dt.bfloat16
I32 = mybir.dt.int32
U32 = mybir.dt.uint32
U8 = mybir.dt.uint8
FP8X4 = mybir.dt.float8_e4m3fn_x4
FP4X4 = mybir.dt.float4_e2m1fn_x4
ALU = mybir.AluOpType
ACT = mybir.ActivationFunctionType

P = 128
BATCH = 2
SEQ = 512
DIM = 512
FEAT = 512
ROPE_BASE = 10000.0
ADD_STEPS = (0, 1, 4, 5, 6, 7)
GPSIMD_STEPS = (3,)
GPSIMD_T = (1, 1, 1, 1, 1, 2, 2, 1)
PACK = 4
F_TILES = FEAT // P
T_TILES = SEQ // P
HALF_T = T_TILES // 2
HALF = SEQ // 2
HALF_TILES = F_TILES // 2
TWO_PI = 2.0 * math.pi

FLOPS = 2 * BATCH * SEQ * DIM * 2 * FEAT


def tile_ropemultiheadattention_pa_kernel(
    tc, x, Wq_words, Wq_scales, bq, Wk_words, Wk_scales, bk, out_0, out_1
):
    nc = tc.nc
    weights = ((Wq_words, Wq_scales, bq, out_0), (Wk_words, Wk_scales, bk, out_1))

    with ExitStack() as ctx:
        ctx.enter_context(tc.manual_schedule())
        keep = ctx.enter_context(tc.tile_pool(name="keep", bufs=1))
        parts = ctx.enter_context(tc.tile_pool(name="parts", bufs=6))
        psum_mx = ctx.enter_context(tc.psum_pool(name="psum_mx", bufs=4))
        psum_tr = ctx.enter_context(tc.psum_pool(name="psum_tr", bufs=4))

        x_sb = [keep.tile([P, T_TILES, DIM], BF16, name="x_sb%d" % b) for b in range(BATCH)]
        grouped = [
            keep.tile([P, SEQ, PACK], BF16, align_bytes=64, name="grouped%d" % b)
            for b in range(BATCH)
        ]
        x_codes = keep.tile([P, BATCH, SEQ], U32, align_bytes=64)
        x_planes = keep.tile([P, BATCH, SEQ], U8, align_bytes=64)
        w_words = keep.tile([P, 2, 2 * FEAT], U8, align_bytes=64)
        w_planes = keep.tile([P, 2, FEAT], U8, align_bytes=64)
        bias = [keep.tile([P, F_TILES], BF16, name="bias%d" % w) for w in range(2)]
        ident = keep.tile([P, P], F32)
        pos = keep.tile([P, SEQ], F32)
        freq_row = keep.tile([P, P], F32)
        table_warmer = keep.tile([P, 1], F32)
        turns = keep.tile([P, HALF_TILES], F32)
        radians = keep.tile([P, HALF_TILES], F32)
        masked_row = keep.tile([P, F_TILES, P], F32)
        whole = keep.tile([P, HALF_TILES, SEQ], I32)
        frac = keep.tile([P, HALF_TILES, SEQ], F32)
        dist = keep.tile([P, F_TILES, SEQ], F32)
        from_low = keep.tile([P, HALF_TILES, 2, SEQ], F32)
        from_high = keep.tile([P, HALF_TILES, 2, SEQ], F32)
        tables = (from_low, from_high)

        def load_x(b, half):
            x_rows = x[b].rearrange("(n t) k -> n t k", t=T_TILES)
            ts = slice(HALF_T * half, HALF_T * (half + 1))
            nc.sync.dma_start(out=x_sb[b][:, ts, :], in_=x_rows[:, ts, :])

        def load_weight(w):
            words, scales = weights[w][0], weights[w][1]
            nc.sync.dma_start(out=w_words[:, w, :].bitcast(I32), in_=words[0].bitcast(I32))
            for quad in range(4):
                nc.sync.dma_start(
                    out=w_planes[32 * quad : 32 * quad + 4, w, :].bitcast(I32),
                    in_=scales[0, 4 * quad : 4 * quad + 4, :].bitcast(I32),
                )

        nc.vector.memset(freq_row[:, 0:2], 1.0)
        nc.scalar.activation(out=table_warmer[:], in_=freq_row[:, 0:1], func=ACT.Sin)
        nc.vector.memset(w_planes[:].rearrange("p w n -> p (w n)").bitcast(I32), 0)
        for width in (2, 8, 32):
            for m in range(1, 4):
                nc.vector.tensor_scalar_mul(
                    out=freq_row[:, m * width : (m + 1) * width],
                    in0=freq_row[:, 0:width],
                    scalar1=ROPE_BASE ** (-(m * width) / FEAT),
                )
        load_x(0, 0)
        for w in range(2):
            load_weight(w)
            with nc.allow_non_contiguous_dma(reason="1 KiB of bias, one element a partition"):
                nc.sync.dma_start(
                    out=bias[w][:], in_=weights[w][2].rearrange("(f p) -> p f", p=P)
                )
        for b, half in ((1, 0), (0, 1), (1, 1)):
            load_x(b, half)

        make_identity(nc, ident[:])
        for half in range(2):
            nc.gpsimd.iota(
                pos[:, (SEQ // 2) * half : (SEQ // 2) * (half + 1)],
                pattern=[[1, T_TILES // 2], [T_TILES, P]],
                base=(T_TILES // 2) * half,
                channel_multiplier=0,
                allow_small_or_imprecise_dtypes=True,
            )

        def per_position(out, f, factor):
            nc.vector.scalar_tensor_tensor(
                out=masked_row[:, f, :], in0=freq_row[:],
                scalar=factor * ROPE_BASE ** (-(f * P) / FEAT), in1=ident[:],
                op0=ALU.mult, op1=ALU.mult, accum_out=out,
            )

        def next_tile_down(out, per_position_above):
            nc.vector.tensor_scalar_mul(
                out=out, in0=per_position_above, scalar1=ROPE_BASE ** (P / FEAT)
            )

        halves = (slice(0, HALF), slice(HALF, SEQ))

        def round_turns(j, cols):
            nc.vector.tensor_scalar(
                out=whole[:, j, cols], in0=pos[:, cols], scalar1=turns[:, j : j + 1], scalar2=0.0,
                op0=ALU.mult, op1=ALU.add,
            )

        def reduce_turns(j, cols):
            nc.vector.scalar_tensor_tensor(
                out=frac[:, j, cols], in0=pos[:, cols], scalar=turns[:, j : j + 1],
                in1=whole[:, j, cols], op0=ALU.mult, op1=ALU.subtract,
            )

        def sine(out, in_, scale, shift=0.0):
            nc.scalar.activation(out=out, in_=in_, func=ACT.Sin, scale=scale, bias=shift)

        def absolute(tiles, cols):
            nc.scalar.activation(
                out=dist[:, tiles, cols], in_=frac[:, tiles, cols], func=ACT.Abs
            )

        def first_tables():
            cols = halves[0]
            sine(from_low[:, 1, 1, cols], pos[:, cols], radians[:, 1:2])
            sine(from_high[:, 1, 1, cols], pos[:, cols], radians[:, 1:2], math.pi / 2.0)
            distance(2, cols, -math.pi / 2.0)
            absolute(1, cols)
            sine(from_low[:, 1, 0, cols], dist[:, 1, cols], -TWO_PI, math.pi / 2.0)
            sine(from_high[:, 1, 0, cols], frac[:, 1, cols], -TWO_PI)
            absolute(0, cols)
            sine(from_low[:, 0, 1, cols], dist[:, 2, cols], -1.0, math.pi / 2.0)
            sine(from_low[:, 0, 0, cols], dist[:, 0, cols], -TWO_PI, math.pi / 2.0)
            distance(3, cols, -math.pi)
            sine(from_high[:, 0, 0, cols], frac[:, 0, cols], -TWO_PI)
            sine(from_high[:, 0, 1, cols], dist[:, 3, cols], 1.0, -math.pi / 2.0)

        def later_tables(lot):
            cols = halves[1]
            low_tiles = slice(0, HALF_TILES)
            if lot == 0:
                sine(from_low[:, 1, 1, cols], pos[:, cols], radians[:, 1:2])
                sine(from_high[:, 1, 1, cols], pos[:, cols], radians[:, 1:2], math.pi / 2.0)
                sine(from_high[:, :, 0, cols], frac[:, low_tiles, cols], -TWO_PI)
            elif lot == 1:
                absolute(low_tiles, cols)
                distance(2, cols, -math.pi / 2.0)
                sine(from_low[:, :, 0, cols], dist[:, low_tiles, cols], -TWO_PI, math.pi / 2.0)
                distance(3, cols, -math.pi)
            else:
                sine(from_low[:, 0, 1, cols], dist[:, 2, cols], -1.0, math.pi / 2.0)
                sine(from_high[:, 0, 1, cols], dist[:, 3, cols], 1.0, -math.pi / 2.0)

        def distance(i, cols, shift):
            nc.scalar.activation(
                out=dist[:, i, cols], in_=pos[:, cols], func=ACT.Abs, scale=radians[:, 0:1],
                bias=shift,
            )

        both_tiles = range(HALF_T)

        def flip_x(b, half, tiles=both_tiles):
            x_words = x_sb[b][:].rearrange("p t k -> p (t k)").bitcast(F32)
            flipped = psum_tr.tile([P, T_TILES, P], F32, tag="tr")
            for tl in tiles:
                first = (DIM // 2) * (2 * half + tl)
                for u in range(2):
                    nc.tensor.transpose(
                        flipped[:, 2 * tl + u, :],
                        x_words[:, first + u : first + DIM // 2 : 2],
                        ident[:],
                    )
            return flipped

        def group_x(copy, b, half, flipped, tiles=both_tiles):
            tiles = slice(tiles.start, tiles.stop)
            grouped_words = (
                grouped[b][:].rearrange("p c t -> p (c t)").bitcast(F32)
                .rearrange("p (h t n u) -> p h t n u", h=2, t=2, u=2)
            )
            copy(
                out=grouped_words[:, half, tiles],
                in_=flipped[:].rearrange("p (t u) n -> p t n u", u=2)[:, tiles],
            )

        def quantise_x(b, half):
            cols = slice((SEQ // 2) * half, (SEQ // 2) * (half + 1))
            nc.vector.quantize_mx(
                out=x_codes[:, b, cols].bitcast(FP8X4),
                scales=x_planes[:, b, cols],
                in_=grouped[b][:, cols, :].rearrange("p c t -> p (c t)"),
            )

        steps = [(half, b, w) for half in range(2) for b in range(BATCH) for w in range(2)]
        last = len(steps) - 1

        def project(s, bank_a_tile=False):
            half, b, w = steps[s]
            cols = halves[half]
            banks = [None, None]
            for j in (1, 0):
                acc = psum_mx.tile([P, 2, HALF], F32, tag="acc")
                sides = [acc[:, 0, :], acc[:, 1, :]]
                if bank_a_tile:
                    other = psum_mx.tile([P, 2, HALF], F32, tag="acc")
                    sides[1] = other[:, 1, :]
                for side in range(2):
                    f = j + side * HALF_TILES
                    nc.tensor.matmul_mx(
                        out=sides[side],
                        lhsT=w_words[:, w, 2 * P * f : 2 * P * (f + 1)].bitcast(FP4X4),
                        lhsT_scale=w_planes[:, w, P * f : P * (f + 1)],
                        rhs=x_codes[:, b, cols].bitcast(FP8X4),
                        rhs_scale=x_planes[:, b, cols],
                        start=True,
                        stop=True,
                    )
                banks[j] = sides
            return banks

        def multiply(s, j, side, acc, product, first=0, last_col=HALF):
            half, b, w = steps[s]
            f = j + side * HALF_TILES
            cols = slice(first, last_col)
            in_table = slice(HALF * half + first, HALF * half + last_col)
            nc.vector.scalar_tensor_tensor(
                out=product[:, :, cols],
                in0=acc[side][:, cols].unsqueeze(1).to_broadcast([P, 2, last_col - first]),
                scalar=bias[w][:, f : f + 1],
                in1=tables[side][:, j, :, in_table], op0=ALU.add, op1=ALU.mult,
            )

        def new_product():
            return parts.tile([P, 2, HALF], F32, name="product", tag="product", bufs=16)

        def multiply_on_gpsimd(s):
            half, b, w = steps[s]
            biased = parts.tile([P, HALF], F32, tag="biased")
            nc.scalar.activation(
                out=biased[:], in_=banks[s][0][1], func=ACT.Identity,
                bias=bias[w][:, HALF_TILES : HALF_TILES + 1],
            )
            product = parts.tile([P, 2, HALF], F32, tag="gpsimd_product")
            nc.gpsimd.tensor_tensor(
                out=product[:], in0=biased[:].unsqueeze(1).to_broadcast([P, 2, HALF]),
                in1=from_high[:, 0, :, halves[half]], op=ALU.mult,
            )
            gpsimd_products[s] = product

        def add_on_gpsimd(summed, pair, tiles):
            nc.gpsimd.tensor_tensor(
                out=summed[:], in0=pair[0][:, :, 0 : P * tiles], in1=pair[1][:, :, 0 : P * tiles],
                op=ALU.add,
            )

        def turn_and_add(slot, pair, h, t):
            cols = slice(P * t, P * (t + 1))
            nc.tensor.matmul(
                out=slot, lhsT=pair[0][:, h, cols], rhs=ident[:],
                is_transpose=True, start=True, stop=False,
            )
            nc.tensor.matmul(
                out=slot, lhsT=pair[1][:, h, cols], rhs=ident[:],
                is_transpose=True, start=False, stop=True,
            )

        def turn_tile(s, t, products, summed, hs=(0, 1)):
            back = psum_tr.tile([P, FEAT], F32, tag="tr")
            for j in (1, 0):
                for h in hs:
                    f = j + h * HALF_TILES
                    slot = back[:, P * f : P * (f + 1)]
                    if summed is not None and j == 1 and t < summed.shape[2] // P:
                        nc.tensor.transpose(slot, summed[:, h, P * t : P * (t + 1)], ident[:])
                    else:
                        turn_and_add(slot, products[j], h, t)
            return back

        def store(s, t, back, copy, features=slice(0, FEAT)):
            half, b, w = steps[s]
            rows = parts.tile([P, FEAT], F32, tag="rows", bufs=12)
            copy(out=rows[:, features], in_=back[:, features])
            out_rows = weights[w][3][b].rearrange("(n t) i -> n t i", t=T_TILES)
            nc.sync.dma_start(
                out=out_rows[:, HALF_T * half + t, features], in_=rows[:, features]
            )

        per_position(turns[:, 1:2], 1, 1.0 / TWO_PI)
        per_position(radians[:, 1:2], 3, 1.0)
        round_turns(1, halves[0])
        next_tile_down(turns[:, 0:1], turns[:, 1:2])
        next_tile_down(radians[:, 0:1], radians[:, 1:2])
        round_turns(0, halves[0])
        reduce_turns(1, halves[0])
        for t in both_tiles:
            one_tile = range(t, t + 1)
            flipped = flip_x(0, 0, one_tile)
            group_x(nc.vector.tensor_copy, 0, 0, flipped, one_tile)
        reduce_turns(0, halves[0])
        first_tables()
        quantise_x(0, 0)
        banks = {0: project(0, True)}
        for j in (1, 0):
            round_turns(j, halves[1])
        for j in (1, 0):
            reduce_turns(j, halves[1])
        flipped = flip_x(1, 0)
        group_x(nc.scalar.copy, 1, 0, flipped)
        later_tables(0)
        banks[1] = project(1)

        gpsimd_products = {}
        if 1 in GPSIMD_STEPS:
            multiply_on_gpsimd(1)
        for s in range(len(steps)):
            products = [[new_product(), new_product()] for j in range(HALF_TILES)]
            if s in GPSIMD_STEPS:
                products[0][1] = gpsimd_products[s]
            summed = None
            if s in ADD_STEPS:
                tiles = GPSIMD_T[s]
                summed = parts.tile([P, 2, tiles * P], F32, name="summed", tag="summed%d" % tiles)
            if s < last:
                for j in (1, 0):
                    if j == 0 and s == 2:
                        quantise_x(steps[s + 2][1], steps[s + 2][0])
                    for side in range(2):
                        if not (s in GPSIMD_STEPS and (j, side) == (0, 1)):
                            multiply(s, j, side, banks[s][j], products[j][side])
                    if j == 1 and summed is not None:
                        add_on_gpsimd(summed, products[1], tiles)
            else:
                for t in range(HALF_T):
                    for j in (1, 0):
                        for side in range(2):
                            multiply(
                                s, j, side, banks[s][j], products[j][side], P * t, P * (t + 1)
                            )
                        if summed is not None and j == 1 and t == 0:
                            add_on_gpsimd(summed, products[1], 1)
            if s + 2 <= last:
                half, b, w = steps[s + 2]
                if w == 0 and s != 2:
                    quantise_x(b, half)
                if s > 0:
                    banks[s + 2] = project(s + 2)
                    if s + 2 in GPSIMD_STEPS:
                        multiply_on_gpsimd(s + 2)
            if s < 2:
                half, b, w = steps[2 * s + 4]
                flipped = flip_x(b, half)
            for t in range(HALF_T):
                if s < last or t < HALF_T - 1:
                    store(s, t, turn_tile(s, t, products, summed), nc.scalar.copy)
                else:
                    for h, copy in enumerate((nc.scalar.copy, nc.vector.tensor_copy)):
                        features = slice(FEAT // 2 * h, FEAT // 2 * (h + 1))
                        store(s, t, turn_tile(s, t, products, summed, (h,)), copy, features)
            if s == 0:
                banks[2] = project(2)
                if 2 in GPSIMD_STEPS:
                    multiply_on_gpsimd(2)
            if s < 2:
                group_x(nc.scalar.copy, b, half, flipped)
            if s < 2:
                later_tables(s + 1)
